import numpy as np
import ml_dtypes

BF16 = ml_dtypes.bfloat16


def bf(x):
    return np.asarray(x, np.float32).astype(BF16)


def f32(x):
    return np.asarray(x, np.float32)


def f64(x):
    return np.asarray(x).astype(np.float64)


def striped(idx):
    return np.tile(idx.reshape(-1, 16).T, (8, 1))


C, S, N, H1, H2, T = 256, 1024, 128, 10, 6, 128


def net(v, w1, b1, w2, b2, w3):
    h = np.tanh(v[:, None, :] * w1[None, :, :] + b1[None, :, :])
    a = np.einsum("rhn,khn->rkn", h, w2) + b2[None, :, :]
    return np.einsum("rkn,kn->rn", np.tanh(a), w3)


def setup_inputs():
    return {"x": f32(np.random.standard_normal((C, S))), "w1": f32(np.random.uniform(0.3, 0.9, (H1, N))), "b1": f32(0.3 * np.random.standard_normal((H1, N))), "w2": f32(np.random.uniform(0.05, 0.45, (H2, H1, N))), "b2": f32(0.3 * np.random.standard_normal((H2, N))), "w3": f32(np.random.uniform(0.2, 0.8, (H2, N))), "offs": striped(np.random.permutation(S)[:N])}


def reference(x, w1, b1, w2, b2, w3, offs):
    idx = offs[:16].T.reshape(-1)
    p = (f64(w1), f64(b1), f64(w2), f64(b2), f64(w3))
    y = net(f64(x)[:, idx], *p)
    grid = np.linspace(-1.0, 1.0, T)
    u = net(np.tile(grid[:, None], (1, N)), *p)
    mean = u.mean(axis=0)
    dev = np.sqrt(((u - mean[None, :]) ** 2).mean(axis=0))
    return (y - mean[None, :]) / dev[None, :]

@@ -1,0 +1,161 @@
+import functools
+
+import concourse.mybir as mybir
+from concourse.masks import make_identity
+
+F32 = mybir.dt.float32
+I32 = mybir.dt.int32
+U16 = mybir.dt.uint16
+MULT = mybir.AluOpType.mult
+ADD = mybir.AluOpType.add
+SUBTRACT = mybir.AluOpType.subtract
+POW = mybir.AluOpType.pow
+TANH = mybir.ActivationFunctionType.Tanh
+INNERMOST = mybir.AxisListType.X
+
+P = 128
+C, S, N, H1, H2, T = 256, 1024, 128, 10, 6, 128
+BLOCKS = C // P
+GROUPS = 16
+Q = N // GROUPS
+HID = H1 * Q
+ROWS = HID + Q
+COLS = Q * H2
+BANK_GROUPS = 8
+ONES_FROM = 64
+
+FLOPS = 2 * (H1 + H1 * H2 + H2) * N * (C + T)
+
+
+def tile_subnetworkblock_kernel(tc, x, w1, b1, w2, b2, w3, offs, out):
+    nc = tc.nc
+    with (
+        tc.tile_pool(name="held", bufs=1) as held,
+        tc.tile_pool(name="work", bufs=3) as work,
+        tc.psum_pool(name="flipped", bufs=2) as flipped,
+        tc.psum_pool(name="banks", bufs=4) as banks,
+        tc.psum_pool(name="stats", bufs=1) as stats,
+    ):
+        offsets = held.tile([P, N // 16], U16, name="offsets")
+        nc.sync.dma_start(offsets[:], offs)
+        x_block = [held.tile([P, S], F32, name=f"x_block{b}") for b in range(BLOCKS)]
+        for b in range(BLOCKS):
+            nc.sync.dma_start(x_block[b][:], x[b * P : (b + 1) * P, :])
+
+        w1_rows = held.tile([P, H1 * N], F32, name="w1_rows")
+        nc.scalar.dma_start(w1_rows[:], w1.rearrange("h j -> (h j)").partition_broadcast(P))
+        w1_col = held.tile([HID, GROUPS], F32, name="w1_col")
+        nc.scalar.dma_start(w1_col[:], w1.rearrange("h (q a) -> (h q) a", a=GROUPS))
+        b1_col = held.tile([HID, GROUPS], F32, name="b1_col")
+        nc.scalar.dma_start(b1_col[:], b1.rearrange("h (q a) -> (h q) a", a=GROUPS))
+        w2_col = held.tile([ROWS, H2, GROUPS], F32, name="w2_col")
+        nc.scalar.dma_start(w2_col[0:HID, :, :], w2.rearrange("k h (q a) -> (h q) k a", a=GROUPS))
+        nc.scalar.dma_start(w2_col[HID:ROWS, :, :], b2.rearrange("k (q a) -> q k a", a=GROUPS))
+        w3_rows = held.tile([P, H2 * N], F32, name="w3_rows")
+        nc.sync.dma_start(w3_rows[:], w3.rearrange("k j -> (k j)").partition_broadcast(P))
+
+        identity = held.tile([P, P], F32, name="identity")
+        make_identity(nc, identity[:])
+        ones = held.tile([P, P], F32, name="ones")
+        nc.vector.memset(ones[:], 1.0)
+        minus_half = held.tile([N, 1], F32, name="minus_half")
+        nc.vector.memset(minus_half[:], -0.5)
+        grid_count = held.tile([HID, T], I32, name="grid_count")
+        nc.gpsimd.iota(grid_count[:], pattern=[[1, T]], base=0, channel_multiplier=0)
+        grid = held.tile([HID, T], F32, name="grid")
+        nc.vector.tensor_scalar(grid[:], grid_count[:], 2.0 / (T - 1), -1.0, op0=MULT, op1=ADD)
+
+        hidden_grid = held.tile([ROWS, GROUPS, T], F32, name="hidden_grid")
+        nc.vector.memset(hidden_grid[ONES_FROM:ROWS, :, :], 1.0)
+        hidden_data = [held.tile([ROWS, GROUPS, P], F32, name=f"hidden_data{b}") for b in range(BLOCKS)]
+        for b in range(BLOCKS):
+            nc.gpsimd.memset(hidden_data[b][ONES_FROM:ROWS, :, :], 1.0)
+
+        same_q = held.tile([ROWS, Q], F32, name="same_q")
+        nc.vector.tensor_reduce(
+            same_q[:], identity[0:ROWS, 0:ROWS].rearrange("p (h q) -> p q h", q=Q), axis=INNERMOST, op=ADD
+        )
+        w2_blocks = held.tile([ROWS, GROUPS * COLS], F32, name="w2_blocks")
+        nc.vector.tensor_tensor(
+            w2_blocks[:].rearrange("p (a q k) -> p a q k", a=GROUPS, q=Q),
+            w2_col[:].rearrange("p k a -> p a k").unsqueeze(2).to_broadcast([ROWS, GROUPS, Q, H2]),
+            same_q[:].unsqueeze(1).unsqueeze(3).to_broadcast([ROWS, GROUPS, Q, H2]),
+            MULT,
+        )
+        w3_columns = held.tile([P, GROUPS * COLS], F32, name="w3_columns")
+        nc.gpsimd.tensor_copy(
+            w3_columns[:].rearrange("p (a q k) -> p a q k", a=GROUPS, q=Q),
+            w3_rows[:].rearrange("p (k q a) -> p a q k", k=H2, q=Q),
+        )
+
+        products = [held.tile([P, H1 * N], F32, name=f"products{b}") for b in range(BLOCKS)]
+        for b in range(BLOCKS):
+            for h in range(H1):
+                nc.vector.tensor_tensor(
+                    products[b][:, h * N : (h + 1) * N],
+                    x_block[b][:].indirect(offsets[:]),
+                    w1_rows[:, h * N : (h + 1) * N],
+                    MULT,
+                )
+
+        def grid_hidden(a):
+            nc.scalar.activation(
+                hidden_grid[0:HID, a, :], grid[:], TANH, bias=b1_col[:, a : a + 1], scale=w1_col[:, a : a + 1]
+            )
+            return hidden_grid[:, a, :]
+
+        def data_hidden(b, a):
+            flipped_products = flipped.tile([HID, P], F32, name="flipped_products")
+            nc.tensor.transpose(
+                flipped_products[:], products[b][:].rearrange("p (m a) -> p a m", a=GROUPS)[:, a, :], identity[:]
+            )
+            nc.scalar.activation(hidden_data[b][0:HID, a, :], flipped_products[:], TANH, bias=b1_col[:, a : a + 1])
+            return hidden_data[b][:, a, :]
+
+        def upper_layers(hidden_of_group):
+            squashed = work.tile([P, GROUPS * COLS], F32, name="squashed")
+            for first in range(0, GROUPS, BANK_GROUPS):
+                bank = banks.tile([P, BANK_GROUPS * COLS], F32, name="bank")
+                for g in range(BANK_GROUPS):
+                    a = first + g
+                    nc.tensor.matmul(
+                        bank[:, g * COLS : (g + 1) * COLS],
+                        lhsT=hidden_of_group(a),
+                        rhs=w2_blocks[:, a * COLS : (a + 1) * COLS],
+                        start=True,
+                        stop=True,
+                    )
+                nc.scalar.activation(squashed[:, first * COLS : (first + BANK_GROUPS) * COLS], bank[:], TANH)
+            weighted = work.tile([P, GROUPS * COLS], F32, name="weighted")
+            nc.vector.tensor_tensor(weighted[:], squashed[:], w3_columns[:], MULT)
+            y = work.tile([P, N], F32, name="y")
+            nc.vector.tensor_reduce(
+                y[:].rearrange("p (q a) -> p q a", q=Q),
+                weighted[:].rearrange("p (a q k) -> p q a k", a=GROUPS, q=Q),
+                axis=INNERMOST,
+                op=ADD,
+            )
+            return y
+
+        u = upper_layers(grid_hidden)
+        u_flipped = stats.tile([N, T], F32, name="u_flipped")
+        nc.tensor.transpose(u_flipped[:], u[:], identity[:])
+        partial = held.tile([N, 6], F32, name="partial")
+        nc.vector.bn_stats(partial[:], u_flipped[:])
+        mean_var = held.tile([N, 2], F32, name="mean_var")
+        nc.vector.bn_aggr(mean_var[:], partial[:])
+        inverse_dev = held.tile([N, 1], F32, name="inverse_dev")
+        nc.gpsimd.tensor_tensor(inverse_dev[:], mean_var[:, 1:2], minus_half[:], POW)
+        diagonals = held.tile([N, 2 * N], F32, name="diagonals")
+        nc.vector.tensor_scalar(diagonals[:, 0:N], identity[:], mean_var[:, 0:1], None, op0=MULT)
+        nc.vector.tensor_scalar(diagonals[:, N : 2 * N], identity[:], inverse_dev[:, 0:1], None, op0=MULT)
+        spread = stats.tile([P, 2 * N], F32, name="spread")
+        nc.tensor.matmul(spread[:], lhsT=ones[:], rhs=diagonals[:], start=True, stop=True)
+
+        for b in range(BLOCKS):
+            y = upper_layers(functools.partial(data_hidden, b))
+            centred = work.tile([P, N], F32, name="centred")
+            nc.vector.tensor_tensor(centred[:], y[:], spread[:, 0:N], SUBTRACT)
+            result = work.tile([P, N], F32, name="result")
+            nc.vector.tensor_tensor(result[:], centred[:], spread[:, N : 2 * N], MULT)
+            nc.sync.dma_start(out[b * P : (b + 1) * P, :], result[:])

@@ -1,5 +1,3 @@
-import functools
-
 import concourse.mybir as mybir
 from concourse.masks import make_identity
 
@@ -21,8 +19,10 @@ Q = N // GROUPS
 HID = H1 * Q
 ROWS = HID + Q
 COLS = Q * H2
+CHUNK = 4
 BANK_GROUPS = 8
 ONES_FROM = 64
+LAG = 2
 
 FLOPS = 2 * (H1 + H1 * H2 + H2) * N * (C + T)
 
@@ -32,44 +32,40 @@ def tile_subnetworkblock_kernel(tc, x, w1, b1, w2, b2, w3, offs, out):
     with (
         tc.tile_pool(name="held", bufs=1) as held,
         tc.tile_pool(name="work", bufs=3) as work,
-        tc.psum_pool(name="flipped", bufs=2) as flipped,
-        tc.psum_pool(name="banks", bufs=4) as banks,
-        tc.psum_pool(name="stats", bufs=1) as stats,
+        tc.psum_pool(name="flipped", bufs=LAG + 1) as flipped,
+        tc.psum_pool(name="banks", bufs=3) as banks,
+        tc.psum_pool(name="rows", bufs=1) as rows,
     ):
         offsets = held.tile([P, N // 16], U16, name="offsets")
         nc.sync.dma_start(offsets[:], offs)
+        w1_rows = held.tile([P, H1 * N], F32, name="w1_rows")
+        nc.sync.dma_start(w1_rows[:], w1.rearrange("h j -> (h j)").partition_broadcast(P))
         x_block = [held.tile([P, S], F32, name=f"x_block{b}") for b in range(BLOCKS)]
         for b in range(BLOCKS):
             nc.sync.dma_start(x_block[b][:], x[b * P : (b + 1) * P, :])
-
-        w1_rows = held.tile([P, H1 * N], F32, name="w1_rows")
-        nc.scalar.dma_start(w1_rows[:], w1.rearrange("h j -> (h j)").partition_broadcast(P))
+        w2_col = held.tile([ROWS, H2, GROUPS], F32, name="w2_col")
+        nc.scalar.dma_start(w2_col[0:HID, :, :], w2.rearrange("k h (q a) -> (h q) k a", a=GROUPS))
+        nc.scalar.dma_start(w2_col[HID:ROWS, :, :], b2.rearrange("k (q a) -> q k a", a=GROUPS))
         w1_col = held.tile([HID, GROUPS], F32, name="w1_col")
         nc.scalar.dma_start(w1_col[:], w1.rearrange("h (q a) -> (h q) a", a=GROUPS))
         b1_col = held.tile([HID, GROUPS], F32, name="b1_col")
         nc.scalar.dma_start(b1_col[:], b1.rearrange("h (q a) -> (h q) a", a=GROUPS))
-        w2_col = held.tile([ROWS, H2, GROUPS], F32, name="w2_col")
-        nc.scalar.dma_start(w2_col[0:HID, :, :], w2.rearrange("k h (q a) -> (h q) k a", a=GROUPS))
-        nc.scalar.dma_start(w2_col[HID:ROWS, :, :], b2.rearrange("k (q a) -> q k a", a=GROUPS))
         w3_rows = held.tile([P, H2 * N], F32, name="w3_rows")
-        nc.sync.dma_start(w3_rows[:], w3.rearrange("k j -> (k j)").partition_broadcast(P))
+        nc.scalar.dma_start(w3_rows[:], w3.rearrange("k j -> (k j)").partition_broadcast(P))
 
         identity = held.tile([P, P], F32, name="identity")
         make_identity(nc, identity[:])
-        ones = held.tile([P, P], F32, name="ones")
-        nc.vector.memset(ones[:], 1.0)
-        minus_half = held.tile([N, 1], F32, name="minus_half")
-        nc.vector.memset(minus_half[:], -0.5)
         grid_count = held.tile([HID, T], I32, name="grid_count")
         nc.gpsimd.iota(grid_count[:], pattern=[[1, T]], base=0, channel_multiplier=0)
         grid = held.tile([HID, T], F32, name="grid")
         nc.vector.tensor_scalar(grid[:], grid_count[:], 2.0 / (T - 1), -1.0, op0=MULT, op1=ADD)
-
-        hidden_grid = held.tile([ROWS, GROUPS, T], F32, name="hidden_grid")
-        nc.vector.memset(hidden_grid[ONES_FROM:ROWS, :, :], 1.0)
-        hidden_data = [held.tile([ROWS, GROUPS, P], F32, name=f"hidden_data{b}") for b in range(BLOCKS)]
-        for b in range(BLOCKS):
-            nc.gpsimd.memset(hidden_data[b][ONES_FROM:ROWS, :, :], 1.0)
+        hidden = [held.tile([ROWS, CHUNK, P], F32, name=f"hidden{i}") for i in range(GROUPS // CHUNK)]
+        for i in range(GROUPS // CHUNK):
+            nc.vector.memset(hidden[i][ONES_FROM:ROWS, :, :], 1.0)
+        ones = held.tile([P, P], F32, name="ones")
+        nc.vector.memset(ones[:], 1.0)
+        minus_half = held.tile([N, 1], F32, name="minus_half")
+        nc.vector.memset(minus_half[:], -0.5)
 
         same_q = held.tile([ROWS, Q], F32, name="same_q")
         nc.vector.tensor_reduce(
@@ -98,64 +94,102 @@ def tile_subnetworkblock_kernel(tc, x, w1, b1, w2, b2, w3, offs, out):
                     MULT,
                 )
 
-        def grid_hidden(a):
-            nc.scalar.activation(
-                hidden_grid[0:HID, a, :], grid[:], TANH, bias=b1_col[:, a : a + 1], scale=w1_col[:, a : a + 1]
-            )
-            return hidden_grid[:, a, :]
+        def second_layer(bank, chunk):
+            for g in range(CHUNK):
+                a = chunk + g
+                nc.tensor.matmul(
+                    bank[:, (a % BANK_GROUPS) * COLS : (a % BANK_GROUPS + 1) * COLS],
+                    lhsT=hidden[chunk // CHUNK][:, g, :],
+                    rhs=w2_blocks[:, a * COLS : (a + 1) * COLS],
+                    start=True,
+                    stop=True,
+                )
 
-        def data_hidden(b, a):
-            flipped_products = flipped.tile([HID, P], F32, name="flipped_products")
-            nc.tensor.transpose(
-                flipped_products[:], products[b][:].rearrange("p (m a) -> p a m", a=GROUPS)[:, a, :], identity[:]
+        def third_layer(bank, first, y):
+            squashed = work.tile([P, BANK_GROUPS * COLS], F32, name="squashed")
+            nc.scalar.activation(squashed[:], bank[:], TANH)
+            weighted = work.tile([P, BANK_GROUPS * COLS], F32, name="weighted")
+            nc.vector.tensor_tensor(
+                weighted[:], squashed[:], w3_columns[:, first * COLS : (first + BANK_GROUPS) * COLS], MULT
             )
-            nc.scalar.activation(hidden_data[b][0:HID, a, :], flipped_products[:], TANH, bias=b1_col[:, a : a + 1])
-            return hidden_data[b][:, a, :]
-
-        def upper_layers(hidden_of_group):
-            squashed = work.tile([P, GROUPS * COLS], F32, name="squashed")
-            for first in range(0, GROUPS, BANK_GROUPS):
-                bank = banks.tile([P, BANK_GROUPS * COLS], F32, name="bank")
-                for g in range(BANK_GROUPS):
-                    a = first + g
-                    nc.tensor.matmul(
-                        bank[:, g * COLS : (g + 1) * COLS],
-                        lhsT=hidden_of_group(a),
-                        rhs=w2_blocks[:, a * COLS : (a + 1) * COLS],
-                        start=True,
-                        stop=True,
-                    )
-                nc.scalar.activation(squashed[:, first * COLS : (first + BANK_GROUPS) * COLS], bank[:], TANH)
-            weighted = work.tile([P, GROUPS * COLS], F32, name="weighted")
-            nc.vector.tensor_tensor(weighted[:], squashed[:], w3_columns[:], MULT)
-            y = work.tile([P, N], F32, name="y")
             nc.vector.tensor_reduce(
-                y[:].rearrange("p (q a) -> p q a", q=Q),
-                weighted[:].rearrange("p (a q k) -> p q a k", a=GROUPS, q=Q),
+                y.rearrange("p (q a) -> p q a", q=Q)[:, :, first : first + BANK_GROUPS],
+                weighted[:].rearrange("p (a q k) -> p q a k", a=BANK_GROUPS, q=Q),
                 axis=INNERMOST,
                 op=ADD,
             )
-            return y
 
-        u = upper_layers(grid_hidden)
-        u_flipped = stats.tile([N, T], F32, name="u_flipped")
-        nc.tensor.transpose(u_flipped[:], u[:], identity[:])
+        u = held.tile([T, N], F32, name="u")
+        for first in range(0, GROUPS, BANK_GROUPS):
+            bank = banks.tile([P, BANK_GROUPS * COLS], F32, name="bank")
+            for chunk in range(first, first + BANK_GROUPS, CHUNK):
+                for g in range(CHUNK):
+                    a = chunk + g
+                    nc.scalar.activation(
+                        hidden[chunk // CHUNK][0:HID, g, :],
+                        grid[:],
+                        TANH,
+                        bias=b1_col[:, a : a + 1],
+                        scale=w1_col[:, a : a + 1],
+                    )
+                second_layer(bank, chunk)
+            third_layer(bank, first, u[:])
+
+        y = held.tile([P, BLOCKS, N], F32, name="y")
+        stream = [(b, chunk) for b in range(BLOCKS) for chunk in range(0, GROUPS, CHUNK)]
+        open_bank = {}
+
+        def step(n):
+            if n < len(stream):
+                b, chunk = stream[n]
+                by_group = products[b][:].rearrange("p (m a) -> p a m", a=GROUPS)
+                flipped_products = flipped.tile([P, CHUNK, P], F32, name="flipped_products")
+                for g in range(CHUNK):
+                    nc.tensor.transpose(flipped_products[0:HID, g, :], by_group[:, chunk + g, :], identity[:])
+                for g in range(CHUNK):
+                    a = chunk + g
+                    nc.scalar.activation(
+                        hidden[chunk // CHUNK][0:HID, g, :],
+                        flipped_products[0:HID, g, :],
+                        TANH,
+                        bias=b1_col[:, a : a + 1],
+                    )
+            if n >= LAG:
+                b, chunk = stream[n - LAG]
+                first = chunk - chunk % BANK_GROUPS
+                if chunk == first:
+                    open_bank[b] = banks.tile([P, BANK_GROUPS * COLS], F32, name="bank")
+                second_layer(open_bank[b], chunk)
+                if chunk == first + BANK_GROUPS - CHUNK:
+                    third_layer(open_bank[b], first, y[:, b, :])
+
+        for n in range(GROUPS // CHUNK + LAG):
+            step(n)
+
+        u_flipped = flipped.tile([P, CHUNK, P], F32, name="flipped_products")
+        nc.tensor.transpose(u_flipped[:, 0, :], u[:], identity[:])
         partial = held.tile([N, 6], F32, name="partial")
-        nc.vector.bn_stats(partial[:], u_flipped[:])
+        nc.vector.bn_stats(partial[:], u_flipped[:, 0, :])
         mean_var = held.tile([N, 2], F32, name="mean_var")
         nc.vector.bn_aggr(mean_var[:], partial[:])
         inverse_dev = held.tile([N, 1], F32, name="inverse_dev")
         nc.gpsimd.tensor_tensor(inverse_dev[:], mean_var[:, 1:2], minus_half[:], POW)
         diagonals = held.tile([N, 2 * N], F32, name="diagonals")
-        nc.vector.tensor_scalar(diagonals[:, 0:N], identity[:], mean_var[:, 0:1], None, op0=MULT)
-        nc.vector.tensor_scalar(diagonals[:, N : 2 * N], identity[:], inverse_dev[:, 0:1], None, op0=MULT)
-        spread = stats.tile([P, 2 * N], F32, name="spread")
+        nc.gpsimd.tensor_scalar(diagonals[:, 0:N], identity[:], mean_var[:, 0:1], None, op0=MULT)
+        nc.gpsimd.tensor_scalar(diagonals[:, N : 2 * N], identity[:], inverse_dev[:, 0:1], None, op0=MULT)
+
+        for n in range(GROUPS // CHUNK + LAG, len(stream) + LAG):
+            step(n)
+
+        spread = rows.tile([P, 2 * N], F32, name="spread")
         nc.tensor.matmul(spread[:], lhsT=ones[:], rhs=diagonals[:], start=True, stop=True)
 
-        for b in range(BLOCKS):
-            y = upper_layers(functools.partial(data_hidden, b))
-            centred = work.tile([P, N], F32, name="centred")
-            nc.vector.tensor_tensor(centred[:], y[:], spread[:, 0:N], SUBTRACT)
-            result = work.tile([P, N], F32, name="result")
-            nc.vector.tensor_tensor(result[:], centred[:], spread[:, N : 2 * N], MULT)
-            nc.sync.dma_start(out[b * P : (b + 1) * P, :], result[:])
+        centred = held.tile([P, BLOCKS, N], F32, name="centred")
+        nc.vector.tensor_tensor(
+            centred[:], y[:], spread[:, 0:N].unsqueeze(1).to_broadcast([P, BLOCKS, N]), SUBTRACT
+        )
+        result = held.tile([P, BLOCKS, N], F32, name="result")
+        nc.vector.tensor_tensor(
+            result[:], centred[:], spread[:, N : 2 * N].unsqueeze(1).to_broadcast([P, BLOCKS, N]), MULT
+        )
+        nc.sync.dma_start(out.rearrange("(b p) j -> p b j", p=P), result[:])

@@ -36,6 +36,16 @@ def tile_subnetworkblock_kernel(tc, x, w1, b1, w2, b2, w3, offs, out):
         tc.psum_pool(name="banks", bufs=3) as banks,
         tc.psum_pool(name="rows", bufs=1) as rows,
     ):
+        w2_col = held.tile([ROWS, H2, GROUPS], F32, name="w2_col")
+        w1_col = held.tile([HID, GROUPS], F32, name="w1_col")
+        b1_col = held.tile([HID, GROUPS], F32, name="b1_col")
+        for low, high in ((0, ONES_FROM), (ONES_FROM, HID)):
+            nc.sync.dma_start(
+                w2_col[low:high, :, :], w2.rearrange("k h (q a) -> (h q) k a", a=GROUPS)[low:high, :, :]
+            )
+            nc.scalar.dma_start(w1_col[low:high, :], w1.rearrange("h (q a) -> (h q) a", a=GROUPS)[low:high, :])
+            nc.scalar.dma_start(b1_col[low:high, :], b1.rearrange("h (q a) -> (h q) a", a=GROUPS)[low:high, :])
+        nc.sync.dma_start(w2_col[HID:ROWS, :, :], b2.rearrange("k (q a) -> q k a", a=GROUPS))
         offsets = held.tile([P, N // 16], U16, name="offsets")
         nc.sync.dma_start(offsets[:], offs)
         w1_rows = held.tile([P, H1 * N], F32, name="w1_rows")
@@ -43,13 +53,6 @@ def tile_subnetworkblock_kernel(tc, x, w1, b1, w2, b2, w3, offs, out):
         x_block = [held.tile([P, S], F32, name=f"x_block{b}") for b in range(BLOCKS)]
         for b in range(BLOCKS):
             nc.sync.dma_start(x_block[b][:], x[b * P : (b + 1) * P, :])
-        w2_col = held.tile([ROWS, H2, GROUPS], F32, name="w2_col")
-        nc.scalar.dma_start(w2_col[0:HID, :, :], w2.rearrange("k h (q a) -> (h q) k a", a=GROUPS))
-        nc.scalar.dma_start(w2_col[HID:ROWS, :, :], b2.rearrange("k (q a) -> q k a", a=GROUPS))
-        w1_col = held.tile([HID, GROUPS], F32, name="w1_col")
-        nc.scalar.dma_start(w1_col[:], w1.rearrange("h (q a) -> (h q) a", a=GROUPS))
-        b1_col = held.tile([HID, GROUPS], F32, name="b1_col")
-        nc.scalar.dma_start(b1_col[:], b1.rearrange("h (q a) -> (h q) a", a=GROUPS))
         w3_rows = held.tile([P, H2 * N], F32, name="w3_rows")
         nc.scalar.dma_start(w3_rows[:], w3.rearrange("k j -> (k j)").partition_broadcast(P))
 
@@ -59,9 +62,9 @@ def tile_subnetworkblock_kernel(tc, x, w1, b1, w2, b2, w3, offs, out):
         nc.gpsimd.iota(grid_count[:], pattern=[[1, T]], base=0, channel_multiplier=0)
         grid = held.tile([HID, T], F32, name="grid")
         nc.vector.tensor_scalar(grid[:], grid_count[:], 2.0 / (T - 1), -1.0, op0=MULT, op1=ADD)
-        hidden = [held.tile([ROWS, CHUNK, P], F32, name=f"hidden{i}") for i in range(GROUPS // CHUNK)]
+        hidden = [held.tile([P, CHUNK, P], F32, name=f"hidden{i}") for i in range(GROUPS // CHUNK)]
         for i in range(GROUPS // CHUNK):
-            nc.vector.memset(hidden[i][ONES_FROM:ROWS, :, :], 1.0)
+            nc.vector.memset(hidden[i][ONES_FROM:P, :, :], 1.0)
         ones = held.tile([P, P], F32, name="ones")
         nc.vector.memset(ones[:], 1.0)
         minus_half = held.tile([N, 1], F32, name="minus_half")
@@ -71,13 +74,19 @@ def tile_subnetworkblock_kernel(tc, x, w1, b1, w2, b2, w3, offs, out):
         nc.vector.tensor_reduce(
             same_q[:], identity[0:ROWS, 0:ROWS].rearrange("p (h q) -> p q h", q=Q), axis=INNERMOST, op=ADD
         )
-        w2_blocks = held.tile([ROWS, GROUPS * COLS], F32, name="w2_blocks")
+        w2_blocks = held.tile([P, GROUPS * COLS], F32, name="w2_blocks")
+        nc.gpsimd.memset(w2_blocks[ONES_FROM:P, :], 0.0)
         nc.vector.tensor_tensor(
-            w2_blocks[:].rearrange("p (a q k) -> p a q k", a=GROUPS, q=Q),
+            w2_blocks[0:ROWS, :].rearrange("p (a q k) -> p a q k", a=GROUPS, q=Q),
             w2_col[:].rearrange("p k a -> p a k").unsqueeze(2).to_broadcast([ROWS, GROUPS, Q, H2]),
             same_q[:].unsqueeze(1).unsqueeze(3).to_broadcast([ROWS, GROUPS, Q, H2]),
             MULT,
         )
+        grid_sums = held.tile([HID, GROUPS, T], F32, name="grid_sums")
+        for a in range(GROUPS):
+            nc.vector.tensor_scalar(
+                grid_sums[:, a, :], grid[:], w1_col[:, a : a + 1], b1_col[:, a : a + 1], op0=MULT, op1=ADD
+            )
         w3_columns = held.tile([P, GROUPS * COLS], F32, name="w3_columns")
         nc.gpsimd.tensor_copy(
             w3_columns[:].rearrange("p (a q k) -> p a q k", a=GROUPS, q=Q),
@@ -123,15 +132,7 @@ def tile_subnetworkblock_kernel(tc, x, w1, b1, w2, b2, w3, offs, out):
         for first in range(0, GROUPS, BANK_GROUPS):
             bank = banks.tile([P, BANK_GROUPS * COLS], F32, name="bank")
             for chunk in range(first, first + BANK_GROUPS, CHUNK):
-                for g in range(CHUNK):
-                    a = chunk + g
-                    nc.scalar.activation(
-                        hidden[chunk // CHUNK][0:HID, g, :],
-                        grid[:],
-                        TANH,
-                        bias=b1_col[:, a : a + 1],
-                        scale=w1_col[:, a : a + 1],
-                    )
+                nc.scalar.activation(hidden[chunk // CHUNK][0:HID, :, :], grid_sums[:, chunk : chunk + CHUNK, :], TANH)
                 second_layer(bank, chunk)
             third_layer(bank, first, u[:])
 

@@ -32,9 +32,6 @@ def tile_subnetworkblock_kernel(tc, x, w1, b1, w2, b2, w3, offs, out):
     with (
         tc.tile_pool(name="held", bufs=1) as held,
         tc.tile_pool(name="work", bufs=3) as work,
-        tc.psum_pool(name="flipped", bufs=LAG + 1) as flipped,
-        tc.psum_pool(name="banks", bufs=3) as banks,
-        tc.psum_pool(name="rows", bufs=1) as rows,
     ):
         w2_col = held.tile([ROWS, H2, GROUPS], F32, name="w2_col")
         w1_col = held.tile([HID, GROUPS], F32, name="w1_col")
@@ -76,16 +73,11 @@ def tile_subnetworkblock_kernel(tc, x, w1, b1, w2, b2, w3, offs, out):
         )
         w2_blocks = held.tile([P, GROUPS * COLS], F32, name="w2_blocks")
         nc.gpsimd.memset(w2_blocks[ONES_FROM:P, :], 0.0)
-        nc.vector.tensor_tensor(
-            w2_blocks[0:ROWS, :].rearrange("p (a q k) -> p a q k", a=GROUPS, q=Q),
-            w2_col[:].rearrange("p k a -> p a k").unsqueeze(2).to_broadcast([ROWS, GROUPS, Q, H2]),
-            same_q[:].unsqueeze(1).unsqueeze(3).to_broadcast([ROWS, GROUPS, Q, H2]),
-            MULT,
-        )
-        grid_sums = held.tile([HID, GROUPS, T], F32, name="grid_sums")
-        for a in range(GROUPS):
-            nc.vector.tensor_scalar(
-                grid_sums[:, a, :], grid[:], w1_col[:, a : a + 1], b1_col[:, a : a + 1], op0=MULT, op1=ADD
+        for q in range(Q):
+            nc.scalar.mul(
+                w2_blocks[0:ROWS, :].rearrange("p (a q k) -> p a q k", a=GROUPS, q=Q)[:, :, q, :],
+                w2_col[:].rearrange("p k a -> p a k"),
+                same_q[:, q : q + 1],
             )
         w3_columns = held.tile([P, GROUPS * COLS], F32, name="w3_columns")
         nc.gpsimd.tensor_copy(
@@ -129,68 +121,84 @@ def tile_subnetworkblock_kernel(tc, x, w1, b1, w2, b2, w3, offs, out):
             )
 
         u = held.tile([T, N], F32, name="u")
-        for first in range(0, GROUPS, BANK_GROUPS):
-            bank = banks.tile([P, BANK_GROUPS * COLS], F32, name="bank")
-            for chunk in range(first, first + BANK_GROUPS, CHUNK):
-                nc.scalar.activation(hidden[chunk // CHUNK][0:HID, :, :], grid_sums[:, chunk : chunk + CHUNK, :], TANH)
-                second_layer(bank, chunk)
-            third_layer(bank, first, u[:])
+        with tc.psum_pool(name="grid_banks", bufs=2) as banks:
+            for first in range(0, GROUPS, BANK_GROUPS):
+                bank = banks.tile([P, BANK_GROUPS * COLS], F32, name="bank")
+                for chunk in range(first, first + BANK_GROUPS, CHUNK):
+                    for g in range(CHUNK):
+                        a = chunk + g
+                        nc.scalar.activation(
+                            hidden[chunk // CHUNK][0:HID, g, :],
+                            grid[:],
+                            TANH,
+                            bias=b1_col[:, a : a + 1],
+                            scale=w1_col[:, a : a + 1],
+                        )
+                    second_layer(bank, chunk)
+                third_layer(bank, first, u[:])
 
-        y = held.tile([P, BLOCKS, N], F32, name="y")
-        stream = [(b, chunk) for b in range(BLOCKS) for chunk in range(0, GROUPS, CHUNK)]
-        open_bank = {}
+        with (
+            tc.psum_pool(name="flipped", bufs=LAG + 1) as flipped,
+            tc.psum_pool(name="banks", bufs=4) as banks,
+            tc.psum_pool(name="rows", bufs=1) as rows,
+        ):
+            y = held.tile([P, BLOCKS, N], F32, name="y")
+            stream = [(b, chunk) for b in range(BLOCKS) for chunk in range(0, GROUPS, CHUNK)]
+            open_bank = {}
 
-        def step(n):
-            if n < len(stream):
-                b, chunk = stream[n]
-                by_group = products[b][:].rearrange("p (m a) -> p a m", a=GROUPS)
-                flipped_products = flipped.tile([P, CHUNK, P], F32, name="flipped_products")
-                for g in range(CHUNK):
-                    nc.tensor.transpose(flipped_products[0:HID, g, :], by_group[:, chunk + g, :], identity[:])
-                for g in range(CHUNK):
-                    a = chunk + g
-                    nc.scalar.activation(
-                        hidden[chunk // CHUNK][0:HID, g, :],
-                        flipped_products[0:HID, g, :],
-                        TANH,
-                        bias=b1_col[:, a : a + 1],
-                    )
-            if n >= LAG:
-                b, chunk = stream[n - LAG]
-                first = chunk - chunk % BANK_GROUPS
-                if chunk == first:
-                    open_bank[b] = banks.tile([P, BANK_GROUPS * COLS], F32, name="bank")
-                second_layer(open_bank[b], chunk)
-                if chunk == first + BANK_GROUPS - CHUNK:
-                    third_layer(open_bank[b], first, y[:, b, :])
+            def step(n):
+                if n < len(stream):
+                    b, chunk = stream[n]
+                    by_group = products[b][:].rearrange("p (m a) -> p a m", a=GROUPS)
+                    flipped_products = flipped.tile([P, CHUNK, P], F32, name="flipped_products")
+                    for g in range(CHUNK):
+                        nc.tensor.transpose(flipped_products[0:HID, g, :], by_group[:, chunk + g, :], identity[:])
+                    for g in range(CHUNK):
+                        a = chunk + g
+                        nc.scalar.activation(
+                            hidden[chunk // CHUNK][0:HID, g, :],
+                            flipped_products[0:HID, g, :],
+                            TANH,
+                            bias=b1_col[:, a : a + 1],
+                        )
+                if n >= LAG:
+                    b, chunk = stream[n - LAG]
+                    first = chunk - chunk % BANK_GROUPS
+                    if chunk == first:
+                        open_bank[b] = banks.tile([P, BANK_GROUPS * COLS], F32, name="bank")
+                    second_layer(open_bank[b], chunk)
+                    if chunk == first + BANK_GROUPS - CHUNK:
+                        third_layer(open_bank[b], first, y[:, b, :])
 
-        for n in range(GROUPS // CHUNK + LAG):
-            step(n)
+            for n in range(GROUPS // CHUNK + LAG):
+                step(n)
 
-        u_flipped = flipped.tile([P, CHUNK, P], F32, name="flipped_products")
-        nc.tensor.transpose(u_flipped[:, 0, :], u[:], identity[:])
-        partial = held.tile([N, 6], F32, name="partial")
-        nc.vector.bn_stats(partial[:], u_flipped[:, 0, :])
-        mean_var = held.tile([N, 2], F32, name="mean_var")
-        nc.vector.bn_aggr(mean_var[:], partial[:])
-        inverse_dev = held.tile([N, 1], F32, name="inverse_dev")
-        nc.gpsimd.tensor_tensor(inverse_dev[:], mean_var[:, 1:2], minus_half[:], POW)
-        diagonals = held.tile([N, 2 * N], F32, name="diagonals")
-        nc.gpsimd.tensor_scalar(diagonals[:, 0:N], identity[:], mean_var[:, 0:1], None, op0=MULT)
-        nc.gpsimd.tensor_scalar(diagonals[:, N : 2 * N], identity[:], inverse_dev[:, 0:1], None, op0=MULT)
+            u_flipped = flipped.tile([P, CHUNK, P], F32, name="flipped_products")
+            nc.tensor.transpose(u_flipped[:, 0, :], u[:], identity[:])
+            partial = held.tile([N, 6], F32, name="partial")
+            nc.vector.bn_stats(partial[:], u_flipped[:, 0, :])
+            mean_var = held.tile([N, 2], F32, name="mean_var")
+            nc.vector.bn_aggr(mean_var[:], partial[:])
+            inverse_dev = held.tile([N, 1], F32, name="inverse_dev")
+            nc.gpsimd.tensor_tensor(inverse_dev[:], mean_var[:, 1:2], minus_half[:], POW)
+            diagonals = held.tile([N, 2 * N], F32, name="diagonals")
+            nc.gpsimd.tensor_scalar(diagonals[:, 0:N], identity[:], mean_var[:, 0:1], None, op0=MULT)
+            nc.gpsimd.tensor_scalar(diagonals[:, N : 2 * N], identity[:], inverse_dev[:, 0:1], None, op0=MULT)
 
-        for n in range(GROUPS // CHUNK + LAG, len(stream) + LAG):
-            step(n)
+            half_way = GROUPS // CHUNK + LAG + GROUPS // CHUNK // 2
+            for n in range(GROUPS // CHUNK + LAG, half_way):
+                step(n)
+            spread = rows.tile([P, 2 * N], F32, name="spread")
+            nc.tensor.matmul(spread[:], lhsT=ones[:], rhs=diagonals[:], start=True, stop=True)
+            for n in range(half_way, len(stream) + LAG):
+                step(n)
 
-        spread = rows.tile([P, 2 * N], F32, name="spread")
-        nc.tensor.matmul(spread[:], lhsT=ones[:], rhs=diagonals[:], start=True, stop=True)
-
-        centred = held.tile([P, BLOCKS, N], F32, name="centred")
-        nc.vector.tensor_tensor(
-            centred[:], y[:], spread[:, 0:N].unsqueeze(1).to_broadcast([P, BLOCKS, N]), SUBTRACT
-        )
-        result = held.tile([P, BLOCKS, N], F32, name="result")
-        nc.vector.tensor_tensor(
-            result[:], centred[:], spread[:, N : 2 * N].unsqueeze(1).to_broadcast([P, BLOCKS, N]), MULT
-        )
-        nc.sync.dma_start(out.rearrange("(b p) j -> p b j", p=P), result[:])
+            centred = held.tile([P, BLOCKS, N], F32, name="centred")
+            nc.vector.tensor_tensor(
+                centred[:], y[:], spread[:, 0:N].unsqueeze(1).to_broadcast([P, BLOCKS, N]), SUBTRACT
+            )
+            result = held.tile([P, BLOCKS, N], F32, name="result")
+            nc.vector.tensor_tensor(
+                result[:], centred[:], spread[:, N : 2 * N].unsqueeze(1).to_broadcast([P, BLOCKS, N]), MULT
+            )
+            nc.sync.dma_start(out.rearrange("(b p) j -> p b j", p=P), result[:])

@@ -1,14 +1,14 @@
 import concourse.mybir as mybir
-from concourse.masks import make_identity
 
 F32 = mybir.dt.float32
-I32 = mybir.dt.int32
 U16 = mybir.dt.uint16
 MULT = mybir.AluOpType.mult
 ADD = mybir.AluOpType.add
 SUBTRACT = mybir.AluOpType.subtract
-POW = mybir.AluOpType.pow
+IS_EQUAL = mybir.AluOpType.is_equal
 TANH = mybir.ActivationFunctionType.Tanh
+COPY = mybir.ActivationFunctionType.Copy
+SQRT = mybir.ActivationFunctionType.Sqrt
 INNERMOST = mybir.AxisListType.X
 
 P = 128
@@ -23,6 +23,7 @@ CHUNK = 4
 BANK_GROUPS = 8
 ONES_FROM = 64
 LAG = 2
+QUADRANT = 32
 
 FLOPS = 2 * (H1 + H1 * H2 + H2) * N * (C + T)
 
@@ -32,17 +33,10 @@ def tile_subnetworkblock_kernel(tc, x, w1, b1, w2, b2, w3, offs, out):
     with (
         tc.tile_pool(name="held", bufs=1) as held,
         tc.tile_pool(name="work", bufs=3) as work,
+        tc.psum_pool(name="flipped", bufs=LAG + 1) as flipped,
+        tc.psum_pool(name="banks", bufs=3) as banks,
+        tc.psum_pool(name="rows", bufs=1) as rows,
     ):
-        w2_col = held.tile([ROWS, H2, GROUPS], F32, name="w2_col")
-        w1_col = held.tile([HID, GROUPS], F32, name="w1_col")
-        b1_col = held.tile([HID, GROUPS], F32, name="b1_col")
-        for low, high in ((0, ONES_FROM), (ONES_FROM, HID)):
-            nc.sync.dma_start(
-                w2_col[low:high, :, :], w2.rearrange("k h (q a) -> (h q) k a", a=GROUPS)[low:high, :, :]
-            )
-            nc.scalar.dma_start(w1_col[low:high, :], w1.rearrange("h (q a) -> (h q) a", a=GROUPS)[low:high, :])
-            nc.scalar.dma_start(b1_col[low:high, :], b1.rearrange("h (q a) -> (h q) a", a=GROUPS)[low:high, :])
-        nc.sync.dma_start(w2_col[HID:ROWS, :, :], b2.rearrange("k (q a) -> q k a", a=GROUPS))
         offsets = held.tile([P, N // 16], U16, name="offsets")
         nc.sync.dma_start(offsets[:], offs)
         w1_rows = held.tile([P, H1 * N], F32, name="w1_rows")
@@ -50,39 +44,53 @@ def tile_subnetworkblock_kernel(tc, x, w1, b1, w2, b2, w3, offs, out):
         x_block = [held.tile([P, S], F32, name=f"x_block{b}") for b in range(BLOCKS)]
         for b in range(BLOCKS):
             nc.sync.dma_start(x_block[b][:], x[b * P : (b + 1) * P, :])
+        w2_col = held.tile([ROWS, H2, GROUPS], F32, name="w2_col")
+        nc.scalar.dma_start(w2_col[0:HID, :, :], w2.rearrange("k h (q a) -> (h q) k a", a=GROUPS))
+        nc.scalar.dma_start(w2_col[HID:ROWS, :, :], b2.rearrange("k (q a) -> q k a", a=GROUPS))
+        w1_col = held.tile([HID, GROUPS], F32, name="w1_col")
+        nc.scalar.dma_start(w1_col[:], w1.rearrange("h (q a) -> (h q) a", a=GROUPS))
+        b1_col = held.tile([HID, GROUPS], F32, name="b1_col")
+        nc.scalar.dma_start(b1_col[:], b1.rearrange("h (q a) -> (h q) a", a=GROUPS))
         w3_rows = held.tile([P, H2 * N], F32, name="w3_rows")
         nc.scalar.dma_start(w3_rows[:], w3.rearrange("k j -> (k j)").partition_broadcast(P))
 
+        ramp = held.tile([P, P], F32, name="ramp", align_bytes=64)
+        nc.vector.memset(ramp[:, 0:1], 0.0)
+        for s in (1, 2, 4, 8, 16, 32, 64):
+            nc.vector.tensor_scalar(ramp[:, s : 2 * s], ramp[:, 0:s], float(s), None, op0=ADD)
+        turned = held.tile([P, QUADRANT], F32, name="turned", align_bytes=64)
+        nc.vector.transpose(turned[:], ramp[:, 0:QUADRANT])
+        partition_index = held.tile([P, 1], F32, name="partition_index")
+        for low in range(0, P, QUADRANT):
+            nc.vector.tensor_scalar(
+                partition_index[low : low + QUADRANT, :], turned[low : low + QUADRANT, 0:1], float(low), None, op0=ADD
+            )
         identity = held.tile([P, P], F32, name="identity")
-        make_identity(nc, identity[:])
-        grid_count = held.tile([HID, T], I32, name="grid_count")
-        nc.gpsimd.iota(grid_count[:], pattern=[[1, T]], base=0, channel_multiplier=0)
+        nc.vector.tensor_scalar(identity[:], ramp[:], partition_index[:, 0:1], None, op0=IS_EQUAL)
         grid = held.tile([HID, T], F32, name="grid")
-        nc.vector.tensor_scalar(grid[:], grid_count[:], 2.0 / (T - 1), -1.0, op0=MULT, op1=ADD)
-        hidden = [held.tile([P, CHUNK, P], F32, name=f"hidden{i}") for i in range(GROUPS // CHUNK)]
+        nc.vector.tensor_scalar(grid[:], ramp[0:HID, :], 2.0 / (T - 1), -1.0, op0=MULT, op1=ADD)
+        hidden = [held.tile([ROWS, CHUNK, P], F32, name=f"hidden{i}") for i in range(GROUPS // CHUNK)]
         for i in range(GROUPS // CHUNK):
-            nc.vector.memset(hidden[i][ONES_FROM:P, :, :], 1.0)
+            nc.vector.memset(hidden[i][ONES_FROM:ROWS, :, :], 1.0)
         ones = held.tile([P, P], F32, name="ones")
         nc.vector.memset(ones[:], 1.0)
-        minus_half = held.tile([N, 1], F32, name="minus_half")
-        nc.vector.memset(minus_half[:], -0.5)
 
         same_q = held.tile([ROWS, Q], F32, name="same_q")
         nc.vector.tensor_reduce(
             same_q[:], identity[0:ROWS, 0:ROWS].rearrange("p (h q) -> p q h", q=Q), axis=INNERMOST, op=ADD
         )
-        w2_blocks = held.tile([P, GROUPS * COLS], F32, name="w2_blocks")
-        nc.gpsimd.memset(w2_blocks[ONES_FROM:P, :], 0.0)
-        for q in range(Q):
-            nc.scalar.mul(
-                w2_blocks[0:ROWS, :].rearrange("p (a q k) -> p a q k", a=GROUPS, q=Q)[:, :, q, :],
-                w2_col[:].rearrange("p k a -> p a k"),
-                same_q[:, q : q + 1],
-            )
+        w2_blocks = held.tile([ROWS, GROUPS * COLS], F32, name="w2_blocks")
+        nc.vector.tensor_tensor(
+            w2_blocks[:].rearrange("p (a q k) -> p a q k", a=GROUPS, q=Q),
+            w2_col[:].rearrange("p k a -> p a k").unsqueeze(2).to_broadcast([ROWS, GROUPS, Q, H2]),
+            same_q[:].unsqueeze(1).unsqueeze(3).to_broadcast([ROWS, GROUPS, Q, H2]),
+            MULT,
+        )
         w3_columns = held.tile([P, GROUPS * COLS], F32, name="w3_columns")
-        nc.gpsimd.tensor_copy(
+        nc.scalar.activation(
             w3_columns[:].rearrange("p (a q k) -> p a q k", a=GROUPS, q=Q),
             w3_rows[:].rearrange("p (k q a) -> p a q k", k=H2, q=Q),
+            COPY,
         )
 
         products = [held.tile([P, H1 * N], F32, name=f"products{b}") for b in range(BLOCKS)]
@@ -121,84 +129,78 @@ def tile_subnetworkblock_kernel(tc, x, w1, b1, w2, b2, w3, offs, out):
             )
 
         u = held.tile([T, N], F32, name="u")
-        with tc.psum_pool(name="grid_banks", bufs=2) as banks:
-            for first in range(0, GROUPS, BANK_GROUPS):
-                bank = banks.tile([P, BANK_GROUPS * COLS], F32, name="bank")
-                for chunk in range(first, first + BANK_GROUPS, CHUNK):
-                    for g in range(CHUNK):
-                        a = chunk + g
-                        nc.scalar.activation(
-                            hidden[chunk // CHUNK][0:HID, g, :],
-                            grid[:],
-                            TANH,
-                            bias=b1_col[:, a : a + 1],
-                            scale=w1_col[:, a : a + 1],
-                        )
-                    second_layer(bank, chunk)
-                third_layer(bank, first, u[:])
+        for first in range(0, GROUPS, BANK_GROUPS):
+            bank = banks.tile([P, BANK_GROUPS * COLS], F32, name="bank")
+            for chunk in range(first, first + BANK_GROUPS, CHUNK):
+                for g in range(CHUNK):
+                    a = chunk + g
+                    nc.scalar.activation(
+                        hidden[chunk // CHUNK][0:HID, g, :],
+                        grid[:],
+                        TANH,
+                        bias=b1_col[:, a : a + 1],
+                        scale=w1_col[:, a : a + 1],
+                    )
+                second_layer(bank, chunk)
+            third_layer(bank, first, u[:])
 
-        with (
-            tc.psum_pool(name="flipped", bufs=LAG + 1) as flipped,
-            tc.psum_pool(name="banks", bufs=4) as banks,
-            tc.psum_pool(name="rows", bufs=1) as rows,
-        ):
-            y = held.tile([P, BLOCKS, N], F32, name="y")
-            stream = [(b, chunk) for b in range(BLOCKS) for chunk in range(0, GROUPS, CHUNK)]
-            open_bank = {}
+        y = held.tile([P, BLOCKS, N], F32, name="y")
+        stream = [(b, chunk) for b in range(BLOCKS) for chunk in range(0, GROUPS, CHUNK)]
+        open_bank = {}
 
-            def step(n):
-                if n < len(stream):
-                    b, chunk = stream[n]
-                    by_group = products[b][:].rearrange("p (m a) -> p a m", a=GROUPS)
-                    flipped_products = flipped.tile([P, CHUNK, P], F32, name="flipped_products")
-                    for g in range(CHUNK):
-                        nc.tensor.transpose(flipped_products[0:HID, g, :], by_group[:, chunk + g, :], identity[:])
-                    for g in range(CHUNK):
-                        a = chunk + g
-                        nc.scalar.activation(
-                            hidden[chunk // CHUNK][0:HID, g, :],
-                            flipped_products[0:HID, g, :],
-                            TANH,
-                            bias=b1_col[:, a : a + 1],
-                        )
-                if n >= LAG:
-                    b, chunk = stream[n - LAG]
-                    first = chunk - chunk % BANK_GROUPS
-                    if chunk == first:
-                        open_bank[b] = banks.tile([P, BANK_GROUPS * COLS], F32, name="bank")
-                    second_layer(open_bank[b], chunk)
-                    if chunk == first + BANK_GROUPS - CHUNK:
-                        third_layer(open_bank[b], first, y[:, b, :])
+        def step(n):
+            if n < len(stream):
+                b, chunk = stream[n]
+                by_group = products[b][:].rearrange("p (m a) -> p a m", a=GROUPS)
+                flipped_products = flipped.tile([P, CHUNK, P], F32, name="flipped_products")
+                for g in range(CHUNK):
+                    nc.tensor.transpose(flipped_products[0:HID, g, :], by_group[:, chunk + g, :], identity[:])
+                for g in range(CHUNK):
+                    a = chunk + g
+                    nc.scalar.activation(
+                        hidden[chunk // CHUNK][0:HID, g, :],
+                        flipped_products[0:HID, g, :],
+                        TANH,
+                        bias=b1_col[:, a : a + 1],
+                    )
+            if n >= LAG:
+                b, chunk = stream[n - LAG]
+                first = chunk - chunk % BANK_GROUPS
+                if chunk == first:
+                    open_bank[b] = banks.tile([P, BANK_GROUPS * COLS], F32, name="bank")
+                second_layer(open_bank[b], chunk)
+                if chunk == first + BANK_GROUPS - CHUNK:
+                    third_layer(open_bank[b], first, y[:, b, :])
 
-            for n in range(GROUPS // CHUNK + LAG):
-                step(n)
+        for n in range(GROUPS // CHUNK + LAG):
+            step(n)
 
-            u_flipped = flipped.tile([P, CHUNK, P], F32, name="flipped_products")
-            nc.tensor.transpose(u_flipped[:, 0, :], u[:], identity[:])
-            partial = held.tile([N, 6], F32, name="partial")
-            nc.vector.bn_stats(partial[:], u_flipped[:, 0, :])
-            mean_var = held.tile([N, 2], F32, name="mean_var")
-            nc.vector.bn_aggr(mean_var[:], partial[:])
-            inverse_dev = held.tile([N, 1], F32, name="inverse_dev")
-            nc.gpsimd.tensor_tensor(inverse_dev[:], mean_var[:, 1:2], minus_half[:], POW)
-            diagonals = held.tile([N, 2 * N], F32, name="diagonals")
-            nc.gpsimd.tensor_scalar(diagonals[:, 0:N], identity[:], mean_var[:, 0:1], None, op0=MULT)
-            nc.gpsimd.tensor_scalar(diagonals[:, N : 2 * N], identity[:], inverse_dev[:, 0:1], None, op0=MULT)
+        u_flipped = flipped.tile([P, CHUNK, P], F32, name="flipped_products")
+        nc.tensor.transpose(u_flipped[:, 0, :], u[:], identity[:])
+        partial = held.tile([N, 6], F32, name="partial")
+        nc.vector.bn_stats(partial[:], u_flipped[:, 0, :])
+        mean_var = held.tile([N, 2], F32, name="mean_var")
+        nc.vector.bn_aggr(mean_var[:], partial[:])
+        deviation = held.tile([N, 1], F32, name="deviation")
+        nc.scalar.activation(deviation[:], mean_var[:, 1:2], SQRT)
+        inverse_dev = held.tile([N, 1], F32, name="inverse_dev")
+        nc.vector.reciprocal(inverse_dev[:], deviation[:])
+        diagonals = held.tile([N, 2 * N], F32, name="diagonals")
+        nc.vector.tensor_scalar(diagonals[:, 0:N], identity[:], mean_var[:, 0:1], None, op0=MULT)
+        nc.vector.tensor_scalar(diagonals[:, N : 2 * N], identity[:], inverse_dev[:, 0:1], None, op0=MULT)
 
-            half_way = GROUPS // CHUNK + LAG + GROUPS // CHUNK // 2
-            for n in range(GROUPS // CHUNK + LAG, half_way):
-                step(n)
-            spread = rows.tile([P, 2 * N], F32, name="spread")
-            nc.tensor.matmul(spread[:], lhsT=ones[:], rhs=diagonals[:], start=True, stop=True)
-            for n in range(half_way, len(stream) + LAG):
-                step(n)
+        for n in range(GROUPS // CHUNK + LAG, len(stream) + LAG):
+            step(n)
 
-            centred = held.tile([P, BLOCKS, N], F32, name="centred")
-            nc.vector.tensor_tensor(
-                centred[:], y[:], spread[:, 0:N].unsqueeze(1).to_broadcast([P, BLOCKS, N]), SUBTRACT
-            )
-            result = held.tile([P, BLOCKS, N], F32, name="result")
-            nc.vector.tensor_tensor(
-                result[:], centred[:], spread[:, N : 2 * N].unsqueeze(1).to_broadcast([P, BLOCKS, N]), MULT
-            )
-            nc.sync.dma_start(out.rearrange("(b p) j -> p b j", p=P), result[:])
+        spread = rows.tile([P, 2 * N], F32, name="spread")
+        nc.tensor.matmul(spread[:], lhsT=ones[:], rhs=diagonals[:], start=True, stop=True)
+
+        centred = held.tile([P, BLOCKS, N], F32, name="centred")
+        nc.vector.tensor_tensor(
+            centred[:], y[:], spread[:, 0:N].unsqueeze(1).to_broadcast([P, BLOCKS, N]), SUBTRACT
+        )
+        result = held.tile([P, BLOCKS, N], F32, name="result")
+        nc.vector.tensor_tensor(
+            result[:], centred[:], spread[:, N : 2 * N].unsqueeze(1).to_broadcast([P, BLOCKS, N]), MULT
+        )
+        nc.sync.dma_start(out.rearrange("(b p) j -> p b j", p=P), result[:])

@@ -7,7 +7,6 @@ ADD = mybir.AluOpType.add
 SUBTRACT = mybir.AluOpType.subtract
 IS_EQUAL = mybir.AluOpType.is_equal
 TANH = mybir.ActivationFunctionType.Tanh
-COPY = mybir.ActivationFunctionType.Copy
 SQRT = mybir.ActivationFunctionType.Sqrt
 INNERMOST = mybir.AxisListType.X
 
@@ -37,6 +36,13 @@ def tile_subnetworkblock_kernel(tc, x, w1, b1, w2, b2, w3, offs, out):
         tc.psum_pool(name="banks", bufs=3) as banks,
         tc.psum_pool(name="rows", bufs=1) as rows,
     ):
+        w2_col = held.tile([ROWS, H2, GROUPS], F32, name="w2_col")
+        nc.sync.dma_start(w2_col[0:HID, :, :], w2.rearrange("k h (q a) -> (h q) k a", a=GROUPS))
+        nc.sync.dma_start(w2_col[HID:ROWS, :, :], b2.rearrange("k (q a) -> q k a", a=GROUPS))
+        w1_col = held.tile([HID, GROUPS], F32, name="w1_col")
+        nc.scalar.dma_start(w1_col[:], w1.rearrange("h (q a) -> (h q) a", a=GROUPS))
+        b1_col = held.tile([HID, GROUPS], F32, name="b1_col")
+        nc.scalar.dma_start(b1_col[:], b1.rearrange("h (q a) -> (h q) a", a=GROUPS))
         offsets = held.tile([P, N // 16], U16, name="offsets")
         nc.sync.dma_start(offsets[:], offs)
         w1_rows = held.tile([P, H1 * N], F32, name="w1_rows")
@@ -44,15 +50,8 @@ def tile_subnetworkblock_kernel(tc, x, w1, b1, w2, b2, w3, offs, out):
         x_block = [held.tile([P, S], F32, name=f"x_block{b}") for b in range(BLOCKS)]
         for b in range(BLOCKS):
             nc.sync.dma_start(x_block[b][:], x[b * P : (b + 1) * P, :])
-        w2_col = held.tile([ROWS, H2, GROUPS], F32, name="w2_col")
-        nc.scalar.dma_start(w2_col[0:HID, :, :], w2.rearrange("k h (q a) -> (h q) k a", a=GROUPS))
-        nc.scalar.dma_start(w2_col[HID:ROWS, :, :], b2.rearrange("k (q a) -> q k a", a=GROUPS))
-        w1_col = held.tile([HID, GROUPS], F32, name="w1_col")
-        nc.scalar.dma_start(w1_col[:], w1.rearrange("h (q a) -> (h q) a", a=GROUPS))
-        b1_col = held.tile([HID, GROUPS], F32, name="b1_col")
-        nc.scalar.dma_start(b1_col[:], b1.rearrange("h (q a) -> (h q) a", a=GROUPS))
         w3_rows = held.tile([P, H2 * N], F32, name="w3_rows")
-        nc.scalar.dma_start(w3_rows[:], w3.rearrange("k j -> (k j)").partition_broadcast(P))
+        nc.sync.dma_start(w3_rows[:], w3.rearrange("k j -> (k j)").partition_broadcast(P))
 
         ramp = held.tile([P, P], F32, name="ramp", align_bytes=64)
         nc.vector.memset(ramp[:, 0:1], 0.0)
@@ -67,14 +66,6 @@ def tile_subnetworkblock_kernel(tc, x, w1, b1, w2, b2, w3, offs, out):
             )
         identity = held.tile([P, P], F32, name="identity")
         nc.vector.tensor_scalar(identity[:], ramp[:], partition_index[:, 0:1], None, op0=IS_EQUAL)
-        grid = held.tile([HID, T], F32, name="grid")
-        nc.vector.tensor_scalar(grid[:], ramp[0:HID, :], 2.0 / (T - 1), -1.0, op0=MULT, op1=ADD)
-        hidden = [held.tile([ROWS, CHUNK, P], F32, name=f"hidden{i}") for i in range(GROUPS // CHUNK)]
-        for i in range(GROUPS // CHUNK):
-            nc.vector.memset(hidden[i][ONES_FROM:ROWS, :, :], 1.0)
-        ones = held.tile([P, P], F32, name="ones")
-        nc.vector.memset(ones[:], 1.0)
-
         same_q = held.tile([ROWS, Q], F32, name="same_q")
         nc.vector.tensor_reduce(
             same_q[:], identity[0:ROWS, 0:ROWS].rearrange("p (h q) -> p q h", q=Q), axis=INNERMOST, op=ADD
@@ -86,12 +77,11 @@ def tile_subnetworkblock_kernel(tc, x, w1, b1, w2, b2, w3, offs, out):
             same_q[:].unsqueeze(1).unsqueeze(3).to_broadcast([ROWS, GROUPS, Q, H2]),
             MULT,
         )
-        w3_columns = held.tile([P, GROUPS * COLS], F32, name="w3_columns")
-        nc.scalar.activation(
-            w3_columns[:].rearrange("p (a q k) -> p a q k", a=GROUPS, q=Q),
-            w3_rows[:].rearrange("p (k q a) -> p a q k", k=H2, q=Q),
-            COPY,
-        )
+        grid = held.tile([HID, T], F32, name="grid")
+        nc.vector.tensor_scalar(grid[:], ramp[0:HID, :], 2.0 / (T - 1), -1.0, op0=MULT, op1=ADD)
+        hidden = [held.tile([ROWS, CHUNK, P], F32, name=f"hidden{i}") for i in range(GROUPS // CHUNK)]
+        for i in range(GROUPS // CHUNK):
+            nc.vector.memset(hidden[i][ONES_FROM:ROWS, :, :], 1.0)
 
         products = [held.tile([P, H1 * N], F32, name=f"products{b}") for b in range(BLOCKS)]
         for b in range(BLOCKS):
@@ -102,6 +92,12 @@ def tile_subnetworkblock_kernel(tc, x, w1, b1, w2, b2, w3, offs, out):
                     w1_rows[:, h * N : (h + 1) * N],
                     MULT,
                 )
+
+        w3_columns = held.tile([P, GROUPS * COLS], F32, name="w3_columns")
+        nc.vector.tensor_copy(
+            w3_columns[:].rearrange("p (a q k) -> p a q k", a=GROUPS, q=Q),
+            w3_rows[:].rearrange("p (k q a) -> p a q k", k=H2, q=Q),
+        )
 
         def second_layer(bank, chunk):
             for g in range(CHUNK):
@@ -185,6 +181,8 @@ def tile_subnetworkblock_kernel(tc, x, w1, b1, w2, b2, w3, offs, out):
         nc.scalar.activation(deviation[:], mean_var[:, 1:2], SQRT)
         inverse_dev = held.tile([N, 1], F32, name="inverse_dev")
         nc.vector.reciprocal(inverse_dev[:], deviation[:])
+        ones = held.tile([P, P], F32, name="ones")
+        nc.vector.memset(ones[:], 1.0)
         diagonals = held.tile([N, 2 * N], F32, name="diagonals")
         nc.vector.tensor_scalar(diagonals[:, 0:N], identity[:], mean_var[:, 0:1], None, op0=MULT)
         nc.vector.tensor_scalar(diagonals[:, N : 2 * N], identity[:], inverse_dev[:, 0:1], None, op0=MULT)

@@ -6,23 +6,27 @@ MULT = mybir.AluOpType.mult
 ADD = mybir.AluOpType.add
 SUBTRACT = mybir.AluOpType.subtract
 IS_EQUAL = mybir.AluOpType.is_equal
+POW = mybir.AluOpType.pow
 TANH = mybir.ActivationFunctionType.Tanh
-SQRT = mybir.ActivationFunctionType.Sqrt
+COPY = mybir.ActivationFunctionType.Copy
 INNERMOST = mybir.AxisListType.X
 
 P = 128
 C, S, N, H1, H2, T = 256, 1024, 128, 10, 6, 128
 BLOCKS = C // P
-GROUPS = 16
-Q = N // GROUPS
+GROUPS = 11
+Q = 12
+PITCH = GROUPS * Q
 HID = H1 * Q
-ROWS = HID + Q
+ROWS = HID + 1
+WIDTH = ROWS * GROUPS
 COLS = Q * H2
-CHUNK = 4
-BANK_GROUPS = 8
-ONES_FROM = 64
+CHUNK = 3
+BANK_GROUPS = 2 * CHUNK
 LAG = 2
 QUADRANT = 32
+PARAMS = 2 + H2
+SATURATING = 20.0
 
 FLOPS = 2 * (H1 + H1 * H2 + H2) * N * (C + T)
 
@@ -31,32 +35,48 @@ def tile_subnetworkblock_kernel(tc, x, w1, b1, w2, b2, w3, offs, out):
     nc = tc.nc
     with (
         tc.tile_pool(name="held", bufs=1) as held,
-        tc.tile_pool(name="work", bufs=3) as work,
-        tc.psum_pool(name="flipped", bufs=LAG + 1) as flipped,
+        tc.tile_pool(name="ring", bufs=12) as ring,
+        tc.tile_pool(name="work", bufs=6) as work,
+        tc.psum_pool(name="flips", bufs=LAG + 1) as flips,
         tc.psum_pool(name="banks", bufs=3) as banks,
-        tc.psum_pool(name="rows", bufs=1) as rows,
+        tc.psum_pool(name="once", bufs=2) as once,
     ):
-        w2_col = held.tile([ROWS, H2, GROUPS], F32, name="w2_col")
-        nc.sync.dma_start(w2_col[0:HID, :, :], w2.rearrange("k h (q a) -> (h q) k a", a=GROUPS))
-        nc.sync.dma_start(w2_col[HID:ROWS, :, :], b2.rearrange("k (q a) -> q k a", a=GROUPS))
-        w1_col = held.tile([HID, GROUPS], F32, name="w1_col")
-        nc.scalar.dma_start(w1_col[:], w1.rearrange("h (q a) -> (h q) a", a=GROUPS))
-        b1_col = held.tile([HID, GROUPS], F32, name="b1_col")
-        nc.scalar.dma_start(b1_col[:], b1.rearrange("h (q a) -> (h q) a", a=GROUPS))
         offsets = held.tile([P, N // 16], U16, name="offsets")
         nc.sync.dma_start(offsets[:], offs)
-        w1_rows = held.tile([P, H1 * N], F32, name="w1_rows")
-        nc.sync.dma_start(w1_rows[:], w1.rearrange("h j -> (h j)").partition_broadcast(P))
+        params = held.tile([PARAMS, WIDTH], F32, name="params")
+        by_unit = params[:, 0 : H1 * PITCH].rearrange("r (h j) -> r h j", j=PITCH)
+        nc.vector.memset(by_unit[:, :, N:PITCH], 1.0)
+        nc.vector.memset(params[:, H1 * PITCH : WIDTH], 0.0)
+        nc.vector.memset(params[0:1, H1 * PITCH : WIDTH], SATURATING)
+        w2_blocks = held.tile([P, H2 * PITCH], F32, name="w2_blocks")
+        nc.vector.memset(w2_blocks[96:P, :].rearrange("p (k j) -> p k j", j=PITCH)[:, :, N:PITCH], 1.0)
+        b2_row = w2_blocks[HID:ROWS, :].rearrange("p (k j) -> p k j", j=PITCH)
+        for h0, h1 in ((0, 8), (8, H1)):
+            nc.sync.dma_start(by_unit[0:1, h0:h1, 0:N], b1[h0:h1, :].unsqueeze(0))
+            nc.sync.dma_start(by_unit[1:2, h0:h1, 0:N], w1[h0:h1, :].unsqueeze(0))
+            for k0, k1 in ((0, 4), (4, H2)):
+                nc.scalar.dma_start(by_unit[2 + k0 : 2 + k1, h0:h1, 0:N], w2[k0:k1, h0:h1, :])
+        for k0, k1 in ((0, 4), (4, H2)):
+            nc.scalar.dma_start(b2_row[:, k0:k1, 0:N], b2[k0:k1, :].unsqueeze(0))
         x_block = [held.tile([P, S], F32, name=f"x_block{b}") for b in range(BLOCKS)]
-        for b in range(BLOCKS):
-            nc.sync.dma_start(x_block[b][:], x[b * P : (b + 1) * P, :])
-        w3_rows = held.tile([P, H2 * N], F32, name="w3_rows")
-        nc.sync.dma_start(w3_rows[:], w3.rearrange("k j -> (k j)").partition_broadcast(P))
+        nc.sync.dma_start(x_block[0][:], x[0:P, :])
+        w1_rows = held.tile([P, H1 * N], F32, name="w1_rows")
+        half = H1 // 2
+        nc.sync.dma_start(w1_rows[:, 0 : half * N], w1[0:half, :].rearrange("h j -> (h j)").partition_broadcast(P))
+        nc.sync.dma_start(w1_rows[:, half * N :], w1[half:H1, :].rearrange("h j -> (h j)").partition_broadcast(P))
+        nc.sync.dma_start(x_block[1][:], x[P : 2 * P, :])
+        w3_rows = held.tile([P, H2 * PITCH], F32, name="w3_rows")
+        w3_by_k = w3_rows[:].rearrange("p (k j) -> p k j", j=PITCH)
+        nc.sync.dma_start(
+            w3_by_k[:, :, 0:N], w3.rearrange("k j -> (k j)").partition_broadcast(P).rearrange("p (k j) -> p k j", j=N)
+        )
 
         ramp = held.tile([P, P], F32, name="ramp", align_bytes=64)
         nc.vector.memset(ramp[:, 0:1], 0.0)
         for s in (1, 2, 4, 8, 16, 32, 64):
             nc.vector.tensor_scalar(ramp[:, s : 2 * s], ramp[:, 0:s], float(s), None, op0=ADD)
+        grid = held.tile([ROWS, T], F32, name="grid")
+        nc.scalar.activation(grid[:], ramp[0:ROWS, :], COPY, bias=-1.0, scale=2.0 / (T - 1))
         turned = held.tile([P, QUADRANT], F32, name="turned", align_bytes=64)
         nc.vector.transpose(turned[:], ramp[:, 0:QUADRANT])
         partition_index = held.tile([P, 1], F32, name="partition_index")
@@ -66,136 +86,149 @@ def tile_subnetworkblock_kernel(tc, x, w1, b1, w2, b2, w3, offs, out):
             )
         identity = held.tile([P, P], F32, name="identity")
         nc.vector.tensor_scalar(identity[:], ramp[:], partition_index[:, 0:1], None, op0=IS_EQUAL)
-        same_q = held.tile([ROWS, Q], F32, name="same_q")
+        same_q = held.tile([HID, Q], F32, name="same_q")
         nc.vector.tensor_reduce(
-            same_q[:], identity[0:ROWS, 0:ROWS].rearrange("p (h q) -> p q h", q=Q), axis=INNERMOST, op=ADD
+            same_q[:], identity[0:HID, 0:HID].rearrange("p (h q) -> p q h", q=Q), axis=INNERMOST, op=ADD
         )
-        w2_blocks = held.tile([ROWS, GROUPS * COLS], F32, name="w2_blocks")
-        nc.vector.tensor_tensor(
-            w2_blocks[:].rearrange("p (a q k) -> p a q k", a=GROUPS, q=Q),
-            w2_col[:].rearrange("p k a -> p a k").unsqueeze(2).to_broadcast([ROWS, GROUPS, Q, H2]),
-            same_q[:].unsqueeze(1).unsqueeze(3).to_broadcast([ROWS, GROUPS, Q, H2]),
-            MULT,
-        )
-        grid = held.tile([HID, T], F32, name="grid")
-        nc.vector.tensor_scalar(grid[:], ramp[0:HID, :], 2.0 / (T - 1), -1.0, op0=MULT, op1=ADD)
-        hidden = [held.tile([ROWS, CHUNK, P], F32, name=f"hidden{i}") for i in range(GROUPS // CHUNK)]
-        for i in range(GROUPS // CHUNK):
-            nc.vector.memset(hidden[i][ONES_FROM:ROWS, :, :], 1.0)
-
-        products = [held.tile([P, H1 * N], F32, name=f"products{b}") for b in range(BLOCKS)]
+        products = [held.tile([P, WIDTH], F32, name=f"products{b}") for b in range(BLOCKS)]
         for b in range(BLOCKS):
+            nc.vector.memset(products[b][:, 0 : H1 * PITCH].rearrange("p (h j) -> p h j", j=PITCH)[:, :, N:PITCH], 0.0)
+            nc.vector.memset(products[b][:, H1 * PITCH : WIDTH], 0.0)
+        nc.vector.memset(w3_by_k[:, :, N:PITCH], 1.0)
+        ones = held.tile([P, P], F32, name="ones")
+        nc.vector.memset(ones[:], 1.0)
+        minus_half = held.tile([N, 1], F32, name="minus_half")
+        nc.vector.memset(minus_half[:], -0.5)
+
+        def look_up(b):
             for h in range(H1):
                 nc.vector.tensor_tensor(
-                    products[b][:, h * N : (h + 1) * N],
+                    products[b][:, h * PITCH : h * PITCH + N],
                     x_block[b][:].indirect(offsets[:]),
                     w1_rows[:, h * N : (h + 1) * N],
                     MULT,
                 )
 
-        w3_columns = held.tile([P, GROUPS * COLS], F32, name="w3_columns")
-        nc.vector.tensor_copy(
-            w3_columns[:].rearrange("p (a q k) -> p a q k", a=GROUPS, q=Q),
-            w3_rows[:].rearrange("p (k q a) -> p a q k", k=H2, q=Q),
-        )
+        look_up(0)
 
-        def second_layer(bank, chunk):
-            for g in range(CHUNK):
-                a = chunk + g
+        params_by_group = params[:].rearrange("r (m a) -> r a m", a=GROUPS)
+        columns_psum = once.tile([ROWS, GROUPS, PARAMS], F32, name="columns_psum", tag="once")
+        for a in range(GROUPS):
+            nc.tensor.matmul(
+                columns_psum[:, a, :],
+                lhsT=params_by_group[:, a, :],
+                rhs=identity[0:PARAMS, 0:PARAMS],
+                start=True,
+                stop=True,
+            )
+        columns = held.tile([ROWS, GROUPS, PARAMS], F32, name="columns")
+        nc.scalar.copy(columns[:], columns_psum[:])
+        nc.vector.tensor_tensor(
+            w2_blocks[0:HID, :].rearrange("p (k q a) -> p k q a", k=H2, q=Q),
+            columns[0:HID, :, 2:PARAMS].rearrange("p a k -> p k a").unsqueeze(2).to_broadcast([HID, H2, Q, GROUPS]),
+            same_q[:].unsqueeze(1).unsqueeze(3).to_broadcast([HID, H2, Q, GROUPS]),
+            MULT,
+        )
+        w2_by_group = w2_blocks[0:ROWS, :].rearrange("p (k q a) -> p a q k", k=H2, q=Q)
+        look_up(1)
+
+        u = held.tile([T, PITCH], F32, name="u")
+        y = held.tile([P, BLOCKS, PITCH], F32, name="y")
+        results = [u[:]] + [y[:, b, :] for b in range(BLOCKS)]
+        stream = [(s, first) for s in range(1 + BLOCKS) for first in range(0, GROUPS, CHUNK)]
+        w3_columns = held.tile([P, GROUPS * COLS], F32, name="w3_columns")
+        hidden_of = {}
+        bank_of = {}
+
+        def first_layer(n):
+            s, first = stream[n]
+            hidden = ring.tile([ROWS, CHUNK, P], F32, name="hidden")
+            hidden_of[n] = hidden
+            group_range = range(first, min(first + CHUNK, GROUPS))
+            if s == 0:
+                for a in group_range:
+                    nc.scalar.activation(
+                        hidden[:, a - first, :], grid[:], TANH, bias=columns[:, a, 0:1], scale=columns[:, a, 1:2]
+                    )
+            else:
+                by_group = products[s - 1][:].rearrange("p (m a) -> p a m", a=GROUPS)
+                flipped = flips.tile([P, CHUNK, P], F32, name="flipped")
+                for a in group_range:
+                    nc.tensor.transpose(flipped[0:ROWS, a - first, :], by_group[:, a, :], identity[:])
+                for a in group_range:
+                    nc.scalar.activation(
+                        hidden[:, a - first, :], flipped[0:ROWS, a - first, :], TANH, bias=columns[:, a, 0:1]
+                    )
+
+        def second_layer(n):
+            s, first = stream[n]
+            start_of_bank = first - first % BANK_GROUPS
+            if first == start_of_bank:
+                bank_of[s] = banks.tile([P, BANK_GROUPS * COLS], F32, name="bank")
+            for a in range(first, min(first + CHUNK, GROUPS)):
                 nc.tensor.matmul(
-                    bank[:, (a % BANK_GROUPS) * COLS : (a % BANK_GROUPS + 1) * COLS],
-                    lhsT=hidden[chunk // CHUNK][:, g, :],
-                    rhs=w2_blocks[:, a * COLS : (a + 1) * COLS],
+                    bank_of[s][:, (a - start_of_bank) * COLS : (a - start_of_bank + 1) * COLS].rearrange(
+                        "p (q k) -> p q k", q=Q
+                    ),
+                    lhsT=hidden_of[n][:, a - first, :],
+                    rhs=w2_by_group[:, a, :, :],
                     start=True,
                     stop=True,
                 )
+            end_of_bank = min(start_of_bank + BANK_GROUPS, GROUPS)
+            if first + CHUNK >= end_of_bank:
+                third_layer(bank_of[s], start_of_bank, end_of_bank - start_of_bank, results[s])
 
-        def third_layer(bank, first, y):
+        def third_layer(bank, first, count, result):
             squashed = work.tile([P, BANK_GROUPS * COLS], F32, name="squashed")
-            nc.scalar.activation(squashed[:], bank[:], TANH)
+            nc.scalar.activation(squashed[:, 0 : count * COLS], bank[:, 0 : count * COLS], TANH)
             weighted = work.tile([P, BANK_GROUPS * COLS], F32, name="weighted")
             nc.vector.tensor_tensor(
-                weighted[:], squashed[:], w3_columns[:, first * COLS : (first + BANK_GROUPS) * COLS], MULT
+                weighted[:, 0 : count * COLS],
+                squashed[:, 0 : count * COLS],
+                w3_columns[:, first * COLS : (first + count) * COLS],
+                MULT,
             )
             nc.vector.tensor_reduce(
-                y.rearrange("p (q a) -> p q a", q=Q)[:, :, first : first + BANK_GROUPS],
-                weighted[:].rearrange("p (a q k) -> p q a k", a=BANK_GROUPS, q=Q),
+                result.rearrange("p (q a) -> p q a", q=Q)[:, :, first : first + count],
+                weighted[:, 0 : count * COLS].rearrange("p (a q k) -> p q a k", a=count, q=Q),
                 axis=INNERMOST,
                 op=ADD,
             )
 
-        u = held.tile([T, N], F32, name="u")
-        for first in range(0, GROUPS, BANK_GROUPS):
-            bank = banks.tile([P, BANK_GROUPS * COLS], F32, name="bank")
-            for chunk in range(first, first + BANK_GROUPS, CHUNK):
-                for g in range(CHUNK):
-                    a = chunk + g
-                    nc.scalar.activation(
-                        hidden[chunk // CHUNK][0:HID, g, :],
-                        grid[:],
-                        TANH,
-                        bias=b1_col[:, a : a + 1],
-                        scale=w1_col[:, a : a + 1],
-                    )
-                second_layer(bank, chunk)
-            third_layer(bank, first, u[:])
-
-        y = held.tile([P, BLOCKS, N], F32, name="y")
-        stream = [(b, chunk) for b in range(BLOCKS) for chunk in range(0, GROUPS, CHUNK)]
-        open_bank = {}
-
-        def step(n):
-            if n < len(stream):
-                b, chunk = stream[n]
-                by_group = products[b][:].rearrange("p (m a) -> p a m", a=GROUPS)
-                flipped_products = flipped.tile([P, CHUNK, P], F32, name="flipped_products")
-                for g in range(CHUNK):
-                    nc.tensor.transpose(flipped_products[0:HID, g, :], by_group[:, chunk + g, :], identity[:])
-                for g in range(CHUNK):
-                    a = chunk + g
-                    nc.scalar.activation(
-                        hidden[chunk // CHUNK][0:HID, g, :],
-                        flipped_products[0:HID, g, :],
-                        TANH,
-                        bias=b1_col[:, a : a + 1],
-                    )
-            if n >= LAG:
-                b, chunk = stream[n - LAG]
-                first = chunk - chunk % BANK_GROUPS
-                if chunk == first:
-                    open_bank[b] = banks.tile([P, BANK_GROUPS * COLS], F32, name="bank")
-                second_layer(open_bank[b], chunk)
-                if chunk == first + BANK_GROUPS - CHUNK:
-                    third_layer(open_bank[b], first, y[:, b, :])
-
-        for n in range(GROUPS // CHUNK + LAG):
-            step(n)
-
-        u_flipped = flipped.tile([P, CHUNK, P], F32, name="flipped_products")
-        nc.tensor.transpose(u_flipped[:, 0, :], u[:], identity[:])
-        partial = held.tile([N, 6], F32, name="partial")
-        nc.vector.bn_stats(partial[:], u_flipped[:, 0, :])
+        chunks_of_a_block = len(stream) // (1 + BLOCKS)
         mean_var = held.tile([N, 2], F32, name="mean_var")
-        nc.vector.bn_aggr(mean_var[:], partial[:])
-        deviation = held.tile([N, 1], F32, name="deviation")
-        nc.scalar.activation(deviation[:], mean_var[:, 1:2], SQRT)
         inverse_dev = held.tile([N, 1], F32, name="inverse_dev")
-        nc.vector.reciprocal(inverse_dev[:], deviation[:])
-        ones = held.tile([P, P], F32, name="ones")
-        nc.vector.memset(ones[:], 1.0)
         diagonals = held.tile([N, 2 * N], F32, name="diagonals")
-        nc.vector.tensor_scalar(diagonals[:, 0:N], identity[:], mean_var[:, 0:1], None, op0=MULT)
-        nc.vector.tensor_scalar(diagonals[:, N : 2 * N], identity[:], inverse_dev[:, 0:1], None, op0=MULT)
-
-        for n in range(GROUPS // CHUNK + LAG, len(stream) + LAG):
-            step(n)
-
-        spread = rows.tile([P, 2 * N], F32, name="spread")
+        for n in range(chunks_of_a_block):
+            first_layer(n)
+        nc.scalar.copy(
+            w3_columns[:].rearrange("p (a q k) -> p a q k", a=GROUPS, q=Q),
+            w3_rows[:].rearrange("p (k q a) -> p a q k", k=H2, q=Q),
+        )
+        for n in range(chunks_of_a_block):
+            second_layer(n)
+        for n in range(chunks_of_a_block, len(stream) + LAG):
+            if n < len(stream):
+                first_layer(n)
+            if n >= chunks_of_a_block + LAG:
+                second_layer(n - LAG)
+            if n == len(stream) - 2:
+                u_flipped = once.tile([N, T], F32, name="u_flipped", tag="once")
+                nc.tensor.transpose(u_flipped[:], u[:, 0:N], identity[:])
+                partial = held.tile([N, 6], F32, name="partial")
+                nc.vector.bn_stats(partial[:], u_flipped[:])
+                nc.vector.bn_aggr(mean_var[:], partial[:])
+                nc.gpsimd.tensor_tensor(inverse_dev[:], mean_var[:, 1:2], minus_half[:], POW)
+            if n == len(stream) - 1:
+                nc.vector.tensor_scalar(diagonals[:, 0:N], identity[:], mean_var[:, 0:1], None, op0=MULT)
+                nc.vector.tensor_scalar(diagonals[:, N : 2 * N], identity[:], inverse_dev[:, 0:1], None, op0=MULT)
+        spread = once.tile([P, 2 * N], F32, name="spread", tag="once")
         nc.tensor.matmul(spread[:], lhsT=ones[:], rhs=diagonals[:], start=True, stop=True)
 
         centred = held.tile([P, BLOCKS, N], F32, name="centred")
         nc.vector.tensor_tensor(
-            centred[:], y[:], spread[:, 0:N].unsqueeze(1).to_broadcast([P, BLOCKS, N]), SUBTRACT
+            centred[:], y[:, :, 0:N], spread[:, 0:N].unsqueeze(1).to_broadcast([P, BLOCKS, N]), SUBTRACT
         )
         result = held.tile([P, BLOCKS, N], F32, name="result")
         nc.vector.tensor_tensor(

@@ -27,6 +27,7 @@ LAG = 2
 QUADRANT = 32
 PARAMS = 2 + H2
 SATURATING = 20.0
+LAST_QUADRANT = 96
 
 FLOPS = 2 * (H1 + H1 * H2 + H2) * N * (C + T)
 
@@ -41,33 +42,31 @@ def tile_subnetworkblock_kernel(tc, x, w1, b1, w2, b2, w3, offs, out):
         tc.psum_pool(name="banks", bufs=3) as banks,
         tc.psum_pool(name="once", bufs=2) as once,
     ):
-        offsets = held.tile([P, N // 16], U16, name="offsets")
-        nc.sync.dma_start(offsets[:], offs)
         params = held.tile([PARAMS, WIDTH], F32, name="params")
         by_unit = params[:, 0 : H1 * PITCH].rearrange("r (h j) -> r h j", j=PITCH)
         nc.vector.memset(by_unit[:, :, N:PITCH], 1.0)
         nc.vector.memset(params[:, H1 * PITCH : WIDTH], 0.0)
         nc.vector.memset(params[0:1, H1 * PITCH : WIDTH], SATURATING)
-        w2_blocks = held.tile([P, H2 * PITCH], F32, name="w2_blocks")
-        nc.vector.memset(w2_blocks[96:P, :].rearrange("p (k j) -> p k j", j=PITCH)[:, :, N:PITCH], 1.0)
-        b2_row = w2_blocks[HID:ROWS, :].rearrange("p (k j) -> p k j", j=PITCH)
         for h0, h1 in ((0, 8), (8, H1)):
             nc.sync.dma_start(by_unit[0:1, h0:h1, 0:N], b1[h0:h1, :].unsqueeze(0))
             nc.sync.dma_start(by_unit[1:2, h0:h1, 0:N], w1[h0:h1, :].unsqueeze(0))
             for k0, k1 in ((0, 4), (4, H2)):
                 nc.scalar.dma_start(by_unit[2 + k0 : 2 + k1, h0:h1, 0:N], w2[k0:k1, h0:h1, :])
+        w2_blocks = held.tile([P, H2 * PITCH], F32, name="w2_blocks")
+        nc.vector.memset(w2_blocks[LAST_QUADRANT:P, :].rearrange("p (k j) -> p k j", j=PITCH)[:, :, N:PITCH], 1.0)
+        b2_row = w2_blocks[HID:ROWS, :].rearrange("p (k j) -> p k j", j=PITCH)
         for k0, k1 in ((0, 4), (4, H2)):
             nc.scalar.dma_start(b2_row[:, k0:k1, 0:N], b2[k0:k1, :].unsqueeze(0))
+        offsets = held.tile([P, N // 16], U16, name="offsets")
+        nc.sync.dma_start(offsets[:], offs)
         x_block = [held.tile([P, S], F32, name=f"x_block{b}") for b in range(BLOCKS)]
-        nc.sync.dma_start(x_block[0][:], x[0:P, :])
         w1_rows = held.tile([P, H1 * N], F32, name="w1_rows")
-        half = H1 // 2
-        nc.sync.dma_start(w1_rows[:, 0 : half * N], w1[0:half, :].rearrange("h j -> (h j)").partition_broadcast(P))
-        nc.sync.dma_start(w1_rows[:, half * N :], w1[half:H1, :].rearrange("h j -> (h j)").partition_broadcast(P))
+        nc.sync.dma_start(x_block[0][:], x[0:P, :])
+        nc.scalar.dma_start(w1_rows[:], w1.rearrange("h j -> (h j)").partition_broadcast(P))
         nc.sync.dma_start(x_block[1][:], x[P : 2 * P, :])
         w3_rows = held.tile([P, H2 * PITCH], F32, name="w3_rows")
         w3_by_k = w3_rows[:].rearrange("p (k j) -> p k j", j=PITCH)
-        nc.sync.dma_start(
+        nc.scalar.dma_start(
             w3_by_k[:, :, 0:N], w3.rearrange("k j -> (k j)").partition_broadcast(P).rearrange("p (k j) -> p k j", j=N)
         )
 
@@ -100,7 +99,34 @@ def tile_subnetworkblock_kernel(tc, x, w1, b1, w2, b2, w3, offs, out):
         minus_half = held.tile([N, 1], F32, name="minus_half")
         nc.vector.memset(minus_half[:], -0.5)
 
-        def look_up(b):
+        chunks = [(first, min(CHUNK, GROUPS - first)) for first in range(0, GROUPS, CHUNK)]
+
+        columns = held.tile([ROWS, GROUPS, 2], F32, name="columns")
+        params_by_group = params[:].rearrange("r (m a) -> r a m", a=GROUPS)
+        for first in range(0, GROUPS, BANK_GROUPS):
+            count = min(BANK_GROUPS, GROUPS - first)
+            flipped_params = once.tile([ROWS, BANK_GROUPS, PARAMS], F32, name="flipped_params", tag="once")
+            for g in range(count):
+                nc.tensor.matmul(
+                    flipped_params[:, g, :],
+                    lhsT=params_by_group[:, first + g, :],
+                    rhs=identity[0:PARAMS, 0:PARAMS],
+                    start=True,
+                    stop=True,
+                )
+            nc.scalar.copy(columns[:, first : first + count, :], flipped_params[:, 0:count, 0:2])
+            nc.vector.tensor_tensor(
+                w2_blocks[0:HID, :].rearrange("p (k q a) -> p k q a", k=H2, q=Q)[:, :, :, first : first + count],
+                flipped_params[0:HID, 0:count, 2:PARAMS]
+                .rearrange("p a k -> p k a")
+                .unsqueeze(2)
+                .to_broadcast([HID, H2, Q, count]),
+                same_q[:].unsqueeze(1).unsqueeze(3).to_broadcast([HID, H2, Q, count]),
+                MULT,
+            )
+        w2_by_group = w2_blocks[0:ROWS, :].rearrange("p (k q a) -> p a q k", k=H2, q=Q)
+
+        for b in range(BLOCKS):
             for h in range(H1):
                 nc.vector.tensor_tensor(
                     products[b][:, h * PITCH : h * PITCH + N],
@@ -109,77 +135,58 @@ def tile_subnetworkblock_kernel(tc, x, w1, b1, w2, b2, w3, offs, out):
                     MULT,
                 )
 
-        look_up(0)
-
-        params_by_group = params[:].rearrange("r (m a) -> r a m", a=GROUPS)
-        columns_psum = once.tile([ROWS, GROUPS, PARAMS], F32, name="columns_psum", tag="once")
-        for a in range(GROUPS):
-            nc.tensor.matmul(
-                columns_psum[:, a, :],
-                lhsT=params_by_group[:, a, :],
-                rhs=identity[0:PARAMS, 0:PARAMS],
-                start=True,
-                stop=True,
-            )
-        columns = held.tile([ROWS, GROUPS, PARAMS], F32, name="columns")
-        nc.scalar.copy(columns[:], columns_psum[:])
-        nc.vector.tensor_tensor(
-            w2_blocks[0:HID, :].rearrange("p (k q a) -> p k q a", k=H2, q=Q),
-            columns[0:HID, :, 2:PARAMS].rearrange("p a k -> p k a").unsqueeze(2).to_broadcast([HID, H2, Q, GROUPS]),
-            same_q[:].unsqueeze(1).unsqueeze(3).to_broadcast([HID, H2, Q, GROUPS]),
-            MULT,
-        )
-        w2_by_group = w2_blocks[0:ROWS, :].rearrange("p (k q a) -> p a q k", k=H2, q=Q)
-        look_up(1)
-
         u = held.tile([T, PITCH], F32, name="u")
         y = held.tile([P, BLOCKS, PITCH], F32, name="y")
         results = [u[:]] + [y[:, b, :] for b in range(BLOCKS)]
-        stream = [(s, first) for s in range(1 + BLOCKS) for first in range(0, GROUPS, CHUNK)]
+        stream = [(s, first, count) for s in range(1 + BLOCKS) for first, count in chunks]
         w3_columns = held.tile([P, GROUPS * COLS], F32, name="w3_columns")
         hidden_of = {}
         bank_of = {}
 
         def first_layer(n):
-            s, first = stream[n]
+            s, first, count = stream[n]
             hidden = ring.tile([ROWS, CHUNK, P], F32, name="hidden")
             hidden_of[n] = hidden
-            group_range = range(first, min(first + CHUNK, GROUPS))
             if s == 0:
-                for a in group_range:
+                for g in range(count):
                     nc.scalar.activation(
-                        hidden[:, a - first, :], grid[:], TANH, bias=columns[:, a, 0:1], scale=columns[:, a, 1:2]
+                        hidden[:, g, :],
+                        grid[:],
+                        TANH,
+                        bias=columns[:, first + g, 0:1],
+                        scale=columns[:, first + g, 1:2],
                     )
             else:
                 by_group = products[s - 1][:].rearrange("p (m a) -> p a m", a=GROUPS)
                 flipped = flips.tile([P, CHUNK, P], F32, name="flipped")
-                for a in group_range:
-                    nc.tensor.transpose(flipped[0:ROWS, a - first, :], by_group[:, a, :], identity[:])
-                for a in group_range:
+                for g in range(count):
+                    nc.tensor.transpose(flipped[0:ROWS, g, :], by_group[:, first + g, :], identity[:])
+                for g in range(count):
                     nc.scalar.activation(
-                        hidden[:, a - first, :], flipped[0:ROWS, a - first, :], TANH, bias=columns[:, a, 0:1]
+                        hidden[:, g, :], flipped[0:ROWS, g, :], TANH, bias=columns[:, first + g, 0:1]
                     )
 
         def second_layer(n):
-            s, first = stream[n]
+            s, first, count = stream[n]
             start_of_bank = first - first % BANK_GROUPS
             if first == start_of_bank:
                 bank_of[s] = banks.tile([P, BANK_GROUPS * COLS], F32, name="bank")
-            for a in range(first, min(first + CHUNK, GROUPS)):
+            for g in range(count):
+                a = first + g
                 nc.tensor.matmul(
                     bank_of[s][:, (a - start_of_bank) * COLS : (a - start_of_bank + 1) * COLS].rearrange(
                         "p (q k) -> p q k", q=Q
                     ),
-                    lhsT=hidden_of[n][:, a - first, :],
+                    lhsT=hidden_of[n][:, g, :],
                     rhs=w2_by_group[:, a, :, :],
                     start=True,
                     stop=True,
                 )
             end_of_bank = min(start_of_bank + BANK_GROUPS, GROUPS)
-            if first + CHUNK >= end_of_bank:
+            if first + count == end_of_bank:
                 third_layer(bank_of[s], start_of_bank, end_of_bank - start_of_bank, results[s])
 
-        def third_layer(bank, first, count, result):
+        def third_layer(bank, first, count, sums):
             squashed = work.tile([P, BANK_GROUPS * COLS], F32, name="squashed")
             nc.scalar.activation(squashed[:, 0 : count * COLS], bank[:, 0 : count * COLS], TANH)
             weighted = work.tile([P, BANK_GROUPS * COLS], F32, name="weighted")
@@ -190,48 +197,51 @@ def tile_subnetworkblock_kernel(tc, x, w1, b1, w2, b2, w3, offs, out):
                 MULT,
             )
             nc.vector.tensor_reduce(
-                result.rearrange("p (q a) -> p q a", q=Q)[:, :, first : first + count],
+                sums.rearrange("p (q a) -> p q a", q=Q)[:, :, first : first + count],
                 weighted[:, 0 : count * COLS].rearrange("p (a q k) -> p q a k", a=count, q=Q),
                 axis=INNERMOST,
                 op=ADD,
             )
 
-        chunks_of_a_block = len(stream) // (1 + BLOCKS)
         mean_var = held.tile([N, 2], F32, name="mean_var")
         inverse_dev = held.tile([N, 1], F32, name="inverse_dev")
-        diagonals = held.tile([N, 2 * N], F32, name="diagonals")
-        for n in range(chunks_of_a_block):
+        constant_rows = held.tile([N, 2, P], F32, name="constant_rows")
+        spread = once.tile([P, 2, N], F32, name="spread", tag="once")
+        last_block = BLOCKS * len(chunks)
+
+        def standardise(b):
+            centred = work.tile([P, N], F32, name="centred")
+            nc.vector.tensor_tensor(centred[:], y[:, b, 0:N], spread[:, 0, :], SUBTRACT)
+            standardised = work.tile([P, N], F32, name="standardised")
+            nc.vector.tensor_tensor(standardised[:], centred[:], spread[:, 1, :], MULT)
+            nc.sync.dma_start(out[b * P : (b + 1) * P, :], standardised[:])
+
+        for n in range(len(chunks)):
             first_layer(n)
         nc.scalar.copy(
             w3_columns[:].rearrange("p (a q k) -> p a q k", a=GROUPS, q=Q),
             w3_rows[:].rearrange("p (k q a) -> p a q k", k=H2, q=Q),
         )
-        for n in range(chunks_of_a_block):
+        for n in range(len(chunks)):
             second_layer(n)
-        for n in range(chunks_of_a_block, len(stream) + LAG):
+        for n in range(len(chunks), len(stream) + LAG):
             if n < len(stream):
                 first_layer(n)
-            if n >= chunks_of_a_block + LAG:
+            if n >= len(chunks) + LAG:
                 second_layer(n - LAG)
-            if n == len(stream) - 2:
+            if n == last_block:
                 u_flipped = once.tile([N, T], F32, name="u_flipped", tag="once")
                 nc.tensor.transpose(u_flipped[:], u[:, 0:N], identity[:])
                 partial = held.tile([N, 6], F32, name="partial")
                 nc.vector.bn_stats(partial[:], u_flipped[:])
                 nc.vector.bn_aggr(mean_var[:], partial[:])
                 nc.gpsimd.tensor_tensor(inverse_dev[:], mean_var[:, 1:2], minus_half[:], POW)
-            if n == len(stream) - 1:
-                nc.vector.tensor_scalar(diagonals[:, 0:N], identity[:], mean_var[:, 0:1], None, op0=MULT)
-                nc.vector.tensor_scalar(diagonals[:, N : 2 * N], identity[:], inverse_dev[:, 0:1], None, op0=MULT)
-        spread = once.tile([P, 2 * N], F32, name="spread", tag="once")
-        nc.tensor.matmul(spread[:], lhsT=ones[:], rhs=diagonals[:], start=True, stop=True)
-
-        centred = held.tile([P, BLOCKS, N], F32, name="centred")
-        nc.vector.tensor_tensor(
-            centred[:], y[:, :, 0:N], spread[:, 0:N].unsqueeze(1).to_broadcast([P, BLOCKS, N]), SUBTRACT
-        )
-        result = held.tile([P, BLOCKS, N], F32, name="result")
-        nc.vector.tensor_tensor(
-            result[:], centred[:], spread[:, N : 2 * N].unsqueeze(1).to_broadcast([P, BLOCKS, N]), MULT
-        )
-        nc.sync.dma_start(out.rearrange("(b p) j -> p b j", p=P), result[:])
+            if n == last_block + 1:
+                nc.vector.tensor_scalar(constant_rows[:, 0, :], ones[:], mean_var[:, 0:1], None, op0=MULT)
+                nc.vector.tensor_scalar(constant_rows[:, 1, :], ones[:], inverse_dev[:, 0:1], None, op0=MULT)
+            if n == last_block + 2:
+                for i in range(2):
+                    nc.tensor.transpose(spread[:, i, :], constant_rows[:, i, :], identity[:])
+            if n == last_block + 3:
+                standardise(0)
+        standardise(1)

@@ -70,10 +70,10 @@ def tile_subnetworkblock_kernel(tc, x, w1, b1, w2, b2, w3, offs, out):
             w3_by_k[:, :, 0:N], w3.rearrange("k j -> (k j)").partition_broadcast(P).rearrange("p (k j) -> p k j", j=N)
         )
 
+        ones = held.tile([P, P], F32, name="ones")
+        nc.vector.memset(ones[:], 1.0)
         ramp = held.tile([P, P], F32, name="ramp", align_bytes=64)
-        nc.vector.memset(ramp[:, 0:1], 0.0)
-        for s in (1, 2, 4, 8, 16, 32, 64):
-            nc.vector.tensor_scalar(ramp[:, s : 2 * s], ramp[:, 0:s], float(s), None, op0=ADD)
+        nc.vector.tensor_tensor_scan(ramp[:], ones[:], ones[:], -1.0, op0=MULT, op1=ADD)
         grid = held.tile([ROWS, T], F32, name="grid")
         nc.scalar.activation(grid[:], ramp[0:ROWS, :], COPY, bias=-1.0, scale=2.0 / (T - 1))
         turned = held.tile([P, QUADRANT], F32, name="turned", align_bytes=64)
@@ -94,8 +94,6 @@ def tile_subnetworkblock_kernel(tc, x, w1, b1, w2, b2, w3, offs, out):
             nc.vector.memset(products[b][:, 0 : H1 * PITCH].rearrange("p (h j) -> p h j", j=PITCH)[:, :, N:PITCH], 0.0)
             nc.vector.memset(products[b][:, H1 * PITCH : WIDTH], 0.0)
         nc.vector.memset(w3_by_k[:, :, N:PITCH], 1.0)
-        ones = held.tile([P, P], F32, name="ones")
-        nc.vector.memset(ones[:], 1.0)
         minus_half = held.tile([N, 1], F32, name="minus_half")
         nc.vector.memset(minus_half[:], -0.5)
 
@@ -229,19 +227,18 @@ def tile_subnetworkblock_kernel(tc, x, w1, b1, w2, b2, w3, offs, out):
                 first_layer(n)
             if n >= len(chunks) + LAG:
                 second_layer(n - LAG)
-            if n == last_block:
+            if n == last_block + 2:
                 u_flipped = once.tile([N, T], F32, name="u_flipped", tag="once")
                 nc.tensor.transpose(u_flipped[:], u[:, 0:N], identity[:])
                 partial = held.tile([N, 6], F32, name="partial")
                 nc.vector.bn_stats(partial[:], u_flipped[:])
                 nc.vector.bn_aggr(mean_var[:], partial[:])
                 nc.gpsimd.tensor_tensor(inverse_dev[:], mean_var[:, 1:2], minus_half[:], POW)
-            if n == last_block + 1:
+            if n == last_block + 3:
                 nc.vector.tensor_scalar(constant_rows[:, 0, :], ones[:], mean_var[:, 0:1], None, op0=MULT)
                 nc.vector.tensor_scalar(constant_rows[:, 1, :], ones[:], inverse_dev[:, 0:1], None, op0=MULT)
-            if n == last_block + 2:
+            if n == last_block + 4:
                 for i in range(2):
                     nc.tensor.transpose(spread[:, i, :], constant_rows[:, i, :], identity[:])
-            if n == last_block + 3:
                 standardise(0)
         standardise(1)

@@ -23,6 +23,7 @@ WIDTH = ROWS * GROUPS
 COLS = Q * H2
 CHUNK = 3
 BANK_GROUPS = 2 * CHUNK
+BANKS = ((0, 2 * CHUNK), (2 * CHUNK, 3 * CHUNK), (3 * CHUNK, GROUPS))
 LAG = 2
 QUADRANT = 32
 PARAMS = 2 + H2
@@ -42,6 +43,11 @@ def tile_subnetworkblock_kernel(tc, x, w1, b1, w2, b2, w3, offs, out):
         tc.psum_pool(name="banks", bufs=3) as banks,
         tc.psum_pool(name="once", bufs=2) as once,
     ):
+        ones = held.tile([P, P], F32, name="ones")
+        nc.vector.memset(ones[:], 1.0)
+        ramp = held.tile([P, P], F32, name="ramp", align_bytes=64)
+        nc.vector.tensor_tensor_scan(ramp[:], ones[:], ones[:], -1.0, op0=MULT, op1=ADD)
+
         params = held.tile([PARAMS, WIDTH], F32, name="params")
         by_unit = params[:, 0 : H1 * PITCH].rearrange("r (h j) -> r h j", j=PITCH)
         nc.vector.memset(by_unit[:, :, N:PITCH], 1.0)
@@ -70,10 +76,6 @@ def tile_subnetworkblock_kernel(tc, x, w1, b1, w2, b2, w3, offs, out):
             w3_by_k[:, :, 0:N], w3.rearrange("k j -> (k j)").partition_broadcast(P).rearrange("p (k j) -> p k j", j=N)
         )
 
-        ones = held.tile([P, P], F32, name="ones")
-        nc.vector.memset(ones[:], 1.0)
-        ramp = held.tile([P, P], F32, name="ramp", align_bytes=64)
-        nc.vector.tensor_tensor_scan(ramp[:], ones[:], ones[:], -1.0, op0=MULT, op1=ADD)
         grid = held.tile([ROWS, T], F32, name="grid")
         nc.scalar.activation(grid[:], ramp[0:ROWS, :], COPY, bias=-1.0, scale=2.0 / (T - 1))
         turned = held.tile([P, QUADRANT], F32, name="turned", align_bytes=64)
@@ -166,7 +168,7 @@ def tile_subnetworkblock_kernel(tc, x, w1, b1, w2, b2, w3, offs, out):
 
         def second_layer(n):
             s, first, count = stream[n]
-            start_of_bank = first - first % BANK_GROUPS
+            start_of_bank, end_of_bank = [(b0, b1) for b0, b1 in BANKS if b0 <= first < b1][0]
             if first == start_of_bank:
                 bank_of[s] = banks.tile([P, BANK_GROUPS * COLS], F32, name="bank")
             for g in range(count):
@@ -180,7 +182,6 @@ def tile_subnetworkblock_kernel(tc, x, w1, b1, w2, b2, w3, offs, out):
                     start=True,
                     stop=True,
                 )
-            end_of_bank = min(start_of_bank + BANK_GROUPS, GROUPS)
             if first + count == end_of_bank:
                 third_layer(bank_of[s], start_of_bank, end_of_bank - start_of_bank, results[s])
 

@@ -80,6 +80,8 @@ def tile_subnetworkblock_kernel(tc, x, w1, b1, w2, b2, w3, offs, out):
         nc.scalar.activation(grid[:], ramp[0:ROWS, :], COPY, bias=-1.0, scale=2.0 / (T - 1))
         turned = held.tile([P, QUADRANT], F32, name="turned", align_bytes=64)
         nc.vector.transpose(turned[:], ramp[:, 0:QUADRANT])
+        small_identity = held.tile([PARAMS, PARAMS], F32, name="small_identity")
+        nc.vector.tensor_scalar(small_identity[:], ramp[0:PARAMS, 0:PARAMS], turned[0:PARAMS, 0:1], None, op0=IS_EQUAL)
         partition_index = held.tile([P, 1], F32, name="partition_index")
         for low in range(0, P, QUADRANT):
             nc.vector.tensor_scalar(
@@ -110,7 +112,7 @@ def tile_subnetworkblock_kernel(tc, x, w1, b1, w2, b2, w3, offs, out):
                 nc.tensor.matmul(
                     flipped_params[:, g, :],
                     lhsT=params_by_group[:, first + g, :],
-                    rhs=identity[0:PARAMS, 0:PARAMS],
+                    rhs=small_identity[:],
                     start=True,
                     stop=True,
                 )
@@ -208,13 +210,6 @@ def tile_subnetworkblock_kernel(tc, x, w1, b1, w2, b2, w3, offs, out):
         spread = once.tile([P, 2, N], F32, name="spread", tag="once")
         last_block = BLOCKS * len(chunks)
 
-        def standardise(b):
-            centred = work.tile([P, N], F32, name="centred")
-            nc.vector.tensor_tensor(centred[:], y[:, b, 0:N], spread[:, 0, :], SUBTRACT)
-            standardised = work.tile([P, N], F32, name="standardised")
-            nc.vector.tensor_tensor(standardised[:], centred[:], spread[:, 1, :], MULT)
-            nc.sync.dma_start(out[b * P : (b + 1) * P, :], standardised[:])
-
         for n in range(len(chunks)):
             first_layer(n)
         nc.scalar.copy(
@@ -238,8 +233,15 @@ def tile_subnetworkblock_kernel(tc, x, w1, b1, w2, b2, w3, offs, out):
             if n == last_block + 3:
                 nc.vector.tensor_scalar(constant_rows[:, 0, :], ones[:], mean_var[:, 0:1], None, op0=MULT)
                 nc.vector.tensor_scalar(constant_rows[:, 1, :], ones[:], inverse_dev[:, 0:1], None, op0=MULT)
-            if n == last_block + 4:
-                for i in range(2):
-                    nc.tensor.transpose(spread[:, i, :], constant_rows[:, i, :], identity[:])
-                standardise(0)
-        standardise(1)
+        for i in range(2):
+            nc.tensor.transpose(spread[:, i, :], constant_rows[:, i, :], identity[:])
+
+        centred = held.tile([P, BLOCKS, N], F32, name="centred")
+        nc.vector.tensor_tensor(
+            centred[:], y[:, :, 0:N], spread[:, 0, :].unsqueeze(1).to_broadcast([P, BLOCKS, N]), SUBTRACT
+        )
+        standardised = held.tile([P, BLOCKS, N], F32, name="standardised")
+        nc.vector.tensor_tensor(
+            standardised[:], centred[:], spread[:, 1, :].unsqueeze(1).to_broadcast([P, BLOCKS, N]), MULT
+        )
+        nc.sync.dma_start(out.rearrange("(b p) j -> p b j", p=P), standardised[:])

@@ -37,6 +37,7 @@ def tile_subnetworkblock_kernel(tc, x, w1, b1, w2, b2, w3, offs, out):
     nc = tc.nc
     with (
         tc.tile_pool(name="held", bufs=1) as held,
+        tc.tile_pool(name="turns", bufs=1) as turns,
         tc.tile_pool(name="ring", bufs=12) as ring,
         tc.tile_pool(name="work", bufs=6) as work,
         tc.psum_pool(name="flips", bufs=LAG + 1) as flips,
@@ -89,59 +90,22 @@ def tile_subnetworkblock_kernel(tc, x, w1, b1, w2, b2, w3, offs, out):
             )
         identity = held.tile([P, P], F32, name="identity")
         nc.vector.tensor_scalar(identity[:], ramp[:], partition_index[:, 0:1], None, op0=IS_EQUAL)
-        same_q = held.tile([HID, Q], F32, name="same_q")
+        same_q = turns.tile([HID, Q], F32, name="same_q", tag="turn")
         nc.vector.tensor_reduce(
             same_q[:], identity[0:HID, 0:HID].rearrange("p (h q) -> p q h", q=Q), axis=INNERMOST, op=ADD
         )
-        products = [held.tile([P, WIDTH], F32, name=f"products{b}") for b in range(BLOCKS)]
-        for b in range(BLOCKS):
-            nc.vector.memset(products[b][:, 0 : H1 * PITCH].rearrange("p (h j) -> p h j", j=PITCH)[:, :, N:PITCH], 0.0)
-            nc.vector.memset(products[b][:, H1 * PITCH : WIDTH], 0.0)
         nc.vector.memset(w3_by_k[:, :, N:PITCH], 1.0)
         minus_half = held.tile([N, 1], F32, name="minus_half")
         nc.vector.memset(minus_half[:], -0.5)
 
         chunks = [(first, min(CHUNK, GROUPS - first)) for first in range(0, GROUPS, CHUNK)]
 
-        columns = held.tile([ROWS, GROUPS, 2], F32, name="columns")
-        params_by_group = params[:].rearrange("r (m a) -> r a m", a=GROUPS)
-        for first in range(0, GROUPS, BANK_GROUPS):
-            count = min(BANK_GROUPS, GROUPS - first)
-            flipped_params = once.tile([ROWS, BANK_GROUPS, PARAMS], F32, name="flipped_params", tag="once")
-            for g in range(count):
-                nc.tensor.matmul(
-                    flipped_params[:, g, :],
-                    lhsT=params_by_group[:, first + g, :],
-                    rhs=small_identity[:],
-                    start=True,
-                    stop=True,
-                )
-            nc.scalar.copy(columns[:, first : first + count, :], flipped_params[:, 0:count, 0:2])
-            nc.vector.tensor_tensor(
-                w2_blocks[0:HID, :].rearrange("p (k q a) -> p k q a", k=H2, q=Q)[:, :, :, first : first + count],
-                flipped_params[0:HID, 0:count, 2:PARAMS]
-                .rearrange("p a k -> p k a")
-                .unsqueeze(2)
-                .to_broadcast([HID, H2, Q, count]),
-                same_q[:].unsqueeze(1).unsqueeze(3).to_broadcast([HID, H2, Q, count]),
-                MULT,
-            )
-        w2_by_group = w2_blocks[0:ROWS, :].rearrange("p (k q a) -> p a q k", k=H2, q=Q)
-
-        for b in range(BLOCKS):
-            for h in range(H1):
-                nc.vector.tensor_tensor(
-                    products[b][:, h * PITCH : h * PITCH + N],
-                    x_block[b][:].indirect(offsets[:]),
-                    w1_rows[:, h * N : (h + 1) * N],
-                    MULT,
-                )
-
         u = held.tile([T, PITCH], F32, name="u")
         y = held.tile([P, BLOCKS, PITCH], F32, name="y")
         results = [u[:]] + [y[:, b, :] for b in range(BLOCKS)]
         stream = [(s, first, count) for s in range(1 + BLOCKS) for first, count in chunks]
         w3_columns = held.tile([P, GROUPS * COLS], F32, name="w3_columns")
+        columns = held.tile([ROWS, GROUPS, 2], F32, name="columns")
         hidden_of = {}
         bank_of = {}
 
@@ -159,7 +123,7 @@ def tile_subnetworkblock_kernel(tc, x, w1, b1, w2, b2, w3, offs, out):
                         scale=columns[:, first + g, 1:2],
                     )
             else:
-                by_group = products[s - 1][:].rearrange("p (m a) -> p a m", a=GROUPS)
+                by_group = products[s - 1].rearrange("p (m a) -> p a m", a=GROUPS)
                 flipped = flips.tile([P, CHUNK, P], F32, name="flipped")
                 for g in range(count):
                     nc.tensor.transpose(flipped[0:ROWS, g, :], by_group[:, first + g, :], identity[:])
@@ -168,11 +132,52 @@ def tile_subnetworkblock_kernel(tc, x, w1, b1, w2, b2, w3, offs, out):
                         hidden[:, g, :], flipped[0:ROWS, g, :], TANH, bias=columns[:, first + g, 0:1]
                     )
 
+        params_by_group = params[:].rearrange("r (m a) -> r a m", a=GROUPS)
+        for first, count in ((0, BANK_GROUPS), (BANK_GROUPS, GROUPS - BANK_GROUPS)):
+            flipped_params = once.tile([ROWS, BANK_GROUPS, PARAMS], F32, name="flipped_params", tag="once")
+            for g in range(count):
+                nc.tensor.matmul(
+                    flipped_params[:, g, :],
+                    lhsT=params_by_group[:, first + g, :],
+                    rhs=small_identity[:],
+                    start=True,
+                    stop=True,
+                )
+            nc.vector.tensor_copy(columns[:, first : first + count, :], flipped_params[:, 0:count, 0:2])
+            nc.vector.tensor_tensor(
+                w2_blocks[0:HID, :].rearrange("p (k q a) -> p k q a", k=H2, q=Q)[:, :, :, first : first + count],
+                flipped_params[0:HID, 0:count, 2:PARAMS]
+                .rearrange("p a k -> p k a")
+                .unsqueeze(2)
+                .to_broadcast([HID, H2, Q, count]),
+                same_q[:].unsqueeze(1).unsqueeze(3).to_broadcast([HID, H2, Q, count]),
+                MULT,
+            )
+            for n in range(len(chunks)):
+                if first <= chunks[n][0] < first + count:
+                    first_layer(n)
+        w2_by_group = w2_blocks[0:ROWS, :].rearrange("p (k q a) -> p a q k", k=H2, q=Q)
+
+        both_products = turns.tile([P, BLOCKS, WIDTH], F32, name="both_products", tag="turn")
+        products = [both_products[:, b, :] for b in range(BLOCKS)]
+        for b in range(BLOCKS):
+            nc.vector.memset(products[b][:, 0 : H1 * PITCH].rearrange("p (h j) -> p h j", j=PITCH)[:, :, N:PITCH], 0.0)
+            nc.vector.memset(products[b][:, H1 * PITCH : WIDTH], 0.0)
+        for b in range(BLOCKS):
+            for h in range(H1):
+                nc.vector.tensor_tensor(
+                    products[b][:, h * PITCH : h * PITCH + N],
+                    x_block[b][:].indirect(offsets[:]),
+                    w1_rows[:, h * N : (h + 1) * N],
+                    MULT,
+                )
+
         def second_layer(n):
             s, first, count = stream[n]
             start_of_bank, end_of_bank = [(b0, b1) for b0, b1 in BANKS if b0 <= first < b1][0]
             if first == start_of_bank:
-                bank_of[s] = banks.tile([P, BANK_GROUPS * COLS], F32, name="bank")
+                pool, name = (flips, "flipped") if s == 0 else (banks, "bank")
+                bank_of[s] = pool.tile([P, BANK_GROUPS * COLS], F32, name=name)
             for g in range(count):
                 a = first + g
                 nc.tensor.matmul(
@@ -208,10 +213,8 @@ def tile_subnetworkblock_kernel(tc, x, w1, b1, w2, b2, w3, offs, out):
         inverse_dev = held.tile([N, 1], F32, name="inverse_dev")
         constant_rows = held.tile([N, 2, P], F32, name="constant_rows")
         spread = once.tile([P, 2, N], F32, name="spread", tag="once")
-        last_block = BLOCKS * len(chunks)
+        flip_of_u = BLOCKS * len(chunks) + 2
 
-        for n in range(len(chunks)):
-            first_layer(n)
         nc.scalar.copy(
             w3_columns[:].rearrange("p (a q k) -> p a q k", a=GROUPS, q=Q),
             w3_rows[:].rearrange("p (k q a) -> p a q k", k=H2, q=Q),
@@ -223,14 +226,14 @@ def tile_subnetworkblock_kernel(tc, x, w1, b1, w2, b2, w3, offs, out):
                 first_layer(n)
             if n >= len(chunks) + LAG:
                 second_layer(n - LAG)
-            if n == last_block + 2:
+            if n == flip_of_u:
                 u_flipped = once.tile([N, T], F32, name="u_flipped", tag="once")
                 nc.tensor.transpose(u_flipped[:], u[:, 0:N], identity[:])
                 partial = held.tile([N, 6], F32, name="partial")
                 nc.vector.bn_stats(partial[:], u_flipped[:])
                 nc.vector.bn_aggr(mean_var[:], partial[:])
                 nc.gpsimd.tensor_tensor(inverse_dev[:], mean_var[:, 1:2], minus_half[:], POW)
-            if n == last_block + 3:
+            if n == flip_of_u + 1:
                 nc.vector.tensor_scalar(constant_rows[:, 0, :], ones[:], mean_var[:, 0:1], None, op0=MULT)
                 nc.vector.tensor_scalar(constant_rows[:, 1, :], ones[:], inverse_dev[:, 0:1], None, op0=MULT)
         for i in range(2):

@@ -18,7 +18,8 @@ GROUPS = 11
 Q = 12
 PITCH = GROUPS * Q
 HID = H1 * Q
-ROWS = HID + 1
+ONE = HID
+ROWS = P
 WIDTH = ROWS * GROUPS
 COLS = Q * H2
 CHUNK = 3
@@ -53,15 +54,15 @@ def tile_subnetworkblock_kernel(tc, x, w1, b1, w2, b2, w3, offs, out):
         by_unit = params[:, 0 : H1 * PITCH].rearrange("r (h j) -> r h j", j=PITCH)
         nc.vector.memset(by_unit[:, :, N:PITCH], 1.0)
         nc.vector.memset(params[:, H1 * PITCH : WIDTH], 0.0)
-        nc.vector.memset(params[0:1, H1 * PITCH : WIDTH], SATURATING)
+        nc.vector.memset(params[0:1, H1 * PITCH : H1 * PITCH + GROUPS], SATURATING)
         for h0, h1 in ((0, 8), (8, H1)):
             nc.sync.dma_start(by_unit[0:1, h0:h1, 0:N], b1[h0:h1, :].unsqueeze(0))
             nc.sync.dma_start(by_unit[1:2, h0:h1, 0:N], w1[h0:h1, :].unsqueeze(0))
             for k0, k1 in ((0, 4), (4, H2)):
                 nc.scalar.dma_start(by_unit[2 + k0 : 2 + k1, h0:h1, 0:N], w2[k0:k1, h0:h1, :])
         w2_blocks = held.tile([P, H2 * PITCH], F32, name="w2_blocks")
-        nc.vector.memset(w2_blocks[LAST_QUADRANT:P, :].rearrange("p (k j) -> p k j", j=PITCH)[:, :, N:PITCH], 1.0)
-        b2_row = w2_blocks[HID:ROWS, :].rearrange("p (k j) -> p k j", j=PITCH)
+        nc.gpsimd.memset(w2_blocks[LAST_QUADRANT:P, :], 0.0)
+        b2_row = w2_blocks[ONE : ONE + 1, :].rearrange("p (k j) -> p k j", j=PITCH)
         for k0, k1 in ((0, 4), (4, H2)):
             nc.scalar.dma_start(b2_row[:, k0:k1, 0:N], b2[k0:k1, :].unsqueeze(0))
         offsets = held.tile([P, N // 16], U16, name="offsets")

import concourse.mybir as mybir

F32 = mybir.dt.float32
U16 = mybir.dt.uint16
MULT = mybir.AluOpType.mult
ADD = mybir.AluOpType.add
SUBTRACT = mybir.AluOpType.subtract
IS_EQUAL = mybir.AluOpType.is_equal
POW = mybir.AluOpType.pow
TANH = mybir.ActivationFunctionType.Tanh
COPY = mybir.ActivationFunctionType.Copy
INNERMOST = mybir.AxisListType.X

P = 128
C, S, N, H1, H2, T = 256, 1024, 128, 10, 6, 128
BLOCKS = C // P
GROUPS = 11
Q = 12
PITCH = GROUPS * Q
HID = H1 * Q
ONE = HID
ROWS = P
WIDTH = ROWS * GROUPS
COLS = Q * H2
CHUNK = 3
BANK_GROUPS = 2 * CHUNK
BANKS = ((0, 2 * CHUNK), (2 * CHUNK, 3 * CHUNK), (3 * CHUNK, GROUPS))
LAG = 2
QUADRANT = 32
PARAMS = 2 + H2
SATURATING = 20.0
LAST_QUADRANT = 96

FLOPS = 2 * (H1 + H1 * H2 + H2) * N * (C + T)


def tile_subnetworkblock_kernel(tc, x, w1, b1, w2, b2, w3, offs, out):
    nc = tc.nc
    with (
        tc.tile_pool(name="held", bufs=1) as held,
        tc.tile_pool(name="turns", bufs=1) as turns,
        tc.tile_pool(name="ring", bufs=12) as ring,
        tc.tile_pool(name="work", bufs=6) as work,
        tc.psum_pool(name="flips", bufs=LAG + 1) as flips,
        tc.psum_pool(name="banks", bufs=3) as banks,
        tc.psum_pool(name="once", bufs=2) as once,
    ):
        ones = held.tile([P, P], F32, name="ones")
        nc.vector.memset(ones[:], 1.0)
        ramp = held.tile([P, P], F32, name="ramp", align_bytes=64)
        nc.vector.tensor_tensor_scan(ramp[:], ones[:], ones[:], -1.0, op0=MULT, op1=ADD)

        params = held.tile([PARAMS, WIDTH], F32, name="params")
        by_unit = params[:, 0 : H1 * PITCH].rearrange("r (h j) -> r h j", j=PITCH)
        nc.vector.memset(by_unit[:, :, N:PITCH], 1.0)
        nc.vector.memset(params[:, H1 * PITCH : WIDTH], 0.0)
        nc.vector.memset(params[0:1, H1 * PITCH : H1 * PITCH + GROUPS], SATURATING)
        for h0, h1 in ((0, 8), (8, H1)):
            nc.sync.dma_start(by_unit[0:1, h0:h1, 0:N], b1[h0:h1, :].unsqueeze(0))
            nc.sync.dma_start(by_unit[1:2, h0:h1, 0:N], w1[h0:h1, :].unsqueeze(0))
            for k0, k1 in ((0, 4), (4, H2)):
                nc.scalar.dma_start(by_unit[2 + k0 : 2 + k1, h0:h1, 0:N], w2[k0:k1, h0:h1, :])
        w2_blocks = held.tile([P, H2 * PITCH], F32, name="w2_blocks")
        nc.gpsimd.memset(w2_blocks[LAST_QUADRANT:P, :], 0.0)
        b2_row = w2_blocks[ONE : ONE + 1, :].rearrange("p (k j) -> p k j", j=PITCH)
        for k0, k1 in ((0, 4), (4, H2)):
            nc.scalar.dma_start(b2_row[:, k0:k1, 0:N], b2[k0:k1, :].unsqueeze(0))
        offsets = held.tile([P, N // 16], U16, name="offsets")
        nc.sync.dma_start(offsets[:], offs)
        x_block = [held.tile([P, S], F32, name=f"x_block{b}") for b in range(BLOCKS)]
        w1_rows = held.tile([P, H1 * N], F32, name="w1_rows")
        nc.sync.dma_start(x_block[0][:], x[0:P, :])
        nc.scalar.dma_start(w1_rows[:], w1.rearrange("h j -> (h j)").partition_broadcast(P))
        nc.sync.dma_start(x_block[1][:], x[P : 2 * P, :])
        w3_rows = held.tile([P, H2 * PITCH], F32, name="w3_rows")
        w3_by_k = w3_rows[:].rearrange("p (k j) -> p k j", j=PITCH)
        nc.scalar.dma_start(
            w3_by_k[:, :, 0:N], w3.rearrange("k j -> (k j)").partition_broadcast(P).rearrange("p (k j) -> p k j", j=N)
        )

        grid = held.tile([ROWS, T], F32, name="grid")
        nc.scalar.activation(grid[:], ramp[0:ROWS, :], COPY, bias=-1.0, scale=2.0 / (T - 1))
        turned = held.tile([P, QUADRANT], F32, name="turned", align_bytes=64)
        nc.vector.transpose(turned[:], ramp[:, 0:QUADRANT])
        small_identity = held.tile([PARAMS, PARAMS], F32, name="small_identity")
        nc.vector.tensor_scalar(small_identity[:], ramp[0:PARAMS, 0:PARAMS], turned[0:PARAMS, 0:1], None, op0=IS_EQUAL)
        partition_index = held.tile([P, 1], F32, name="partition_index")
        for low in range(0, P, QUADRANT):
            nc.vector.tensor_scalar(
                partition_index[low : low + QUADRANT, :], turned[low : low + QUADRANT, 0:1], float(low), None, op0=ADD
            )
        identity = held.tile([P, P], F32, name="identity")
        nc.vector.tensor_scalar(identity[:], ramp[:], partition_index[:, 0:1], None, op0=IS_EQUAL)
        same_q = turns.tile([HID, Q], F32, name="same_q", tag="turn")
        nc.vector.tensor_reduce(
            same_q[:], identity[0:HID, 0:HID].rearrange("p (h q) -> p q h", q=Q), axis=INNERMOST, op=ADD
        )
        nc.vector.memset(w3_by_k[:, :, N:PITCH], 1.0)
        minus_half = held.tile([N, 1], F32, name="minus_half")
        nc.vector.memset(minus_half[:], -0.5)

        chunks = [(first, min(CHUNK, GROUPS - first)) for first in range(0, GROUPS, CHUNK)]

        u = held.tile([T, PITCH], F32, name="u")
        y = held.tile([P, BLOCKS, PITCH], F32, name="y")
        results = [u[:]] + [y[:, b, :] for b in range(BLOCKS)]
        stream = [(s, first, count) for s in range(1 + BLOCKS) for first, count in chunks]
        w3_columns = held.tile([P, GROUPS * COLS], F32, name="w3_columns")
        columns = held.tile([ROWS, GROUPS, 2], F32, name="columns")
        hidden_of = {}
        bank_of = {}

        def first_layer(n):
            s, first, count = stream[n]
            hidden = ring.tile([ROWS, CHUNK, P], F32, name="hidden")
            hidden_of[n] = hidden
            if s == 0:
                for g in range(count):
                    nc.scalar.activation(
                        hidden[:, g, :],
                        grid[:],
                        TANH,
                        bias=columns[:, first + g, 0:1],
                        scale=columns[:, first + g, 1:2],
                    )
            else:
                by_group = products[s - 1].rearrange("p (m a) -> p a m", a=GROUPS)
                flipped = flips.tile([P, CHUNK, P], F32, name="flipped")
                for g in range(count):
                    nc.tensor.transpose(flipped[0:ROWS, g, :], by_group[:, first + g, :], identity[:])
                for g in range(count):
                    nc.scalar.activation(
                        hidden[:, g, :], flipped[0:ROWS, g, :], TANH, bias=columns[:, first + g, 0:1]
                    )

        params_by_group = params[:].rearrange("r (m a) -> r a m", a=GROUPS)
        for first, count in ((0, BANK_GROUPS), (BANK_GROUPS, GROUPS - BANK_GROUPS)):
            flipped_params = once.tile([ROWS, BANK_GROUPS, PARAMS], F32, name="flipped_params", tag="once")
            for g in range(count):
                nc.tensor.matmul(
                    flipped_params[:, g, :],
                    lhsT=params_by_group[:, first + g, :],
                    rhs=small_identity[:],
                    start=True,
                    stop=True,
                )
            nc.vector.tensor_copy(columns[:, first : first + count, :], flipped_params[:, 0:count, 0:2])
            nc.vector.tensor_tensor(
                w2_blocks[0:HID, :].rearrange("p (k q a) -> p k q a", k=H2, q=Q)[:, :, :, first : first + count],
                flipped_params[0:HID, 0:count, 2:PARAMS]
                .rearrange("p a k -> p k a")
                .unsqueeze(2)
                .to_broadcast([HID, H2, Q, count]),
                same_q[:].unsqueeze(1).unsqueeze(3).to_broadcast([HID, H2, Q, count]),
                MULT,
            )
            for n in range(len(chunks)):
                if first <= chunks[n][0] < first + count:
                    first_layer(n)
        w2_by_group = w2_blocks[0:ROWS, :].rearrange("p (k q a) -> p a q k", k=H2, q=Q)

        both_products = turns.tile([P, BLOCKS, WIDTH], F32, name="both_products", tag="turn")
        products = [both_products[:, b, :] for b in range(BLOCKS)]
        for b in range(BLOCKS):
            nc.vector.memset(products[b][:, 0 : H1 * PITCH].rearrange("p (h j) -> p h j", j=PITCH)[:, :, N:PITCH], 0.0)
            nc.vector.memset(products[b][:, H1 * PITCH : WIDTH], 0.0)
        for b in range(BLOCKS):
            for h in range(H1):
                nc.vector.tensor_tensor(
                    products[b][:, h * PITCH : h * PITCH + N],
                    x_block[b][:].indirect(offsets[:]),
                    w1_rows[:, h * N : (h + 1) * N],
                    MULT,
                )

        def second_layer(n):
            s, first, count = stream[n]
            start_of_bank, end_of_bank = [(b0, b1) for b0, b1 in BANKS if b0 <= first < b1][0]
            if first == start_of_bank:
                pool, name = (flips, "flipped") if s == 0 else (banks, "bank")
                bank_of[s] = pool.tile([P, BANK_GROUPS * COLS], F32, name=name)
            for g in range(count):
                a = first + g
                nc.tensor.matmul(
                    bank_of[s][:, (a - start_of_bank) * COLS : (a - start_of_bank + 1) * COLS].rearrange(
                        "p (q k) -> p q k", q=Q
                    ),
                    lhsT=hidden_of[n][:, g, :],
                    rhs=w2_by_group[:, a, :, :],
                    start=True,
                    stop=True,
                )
            if first + count == end_of_bank:
                third_layer(bank_of[s], start_of_bank, end_of_bank - start_of_bank, results[s])

        def third_layer(bank, first, count, sums):
            squashed = work.tile([P, BANK_GROUPS * COLS], F32, name="squashed")
            nc.scalar.activation(squashed[:, 0 : count * COLS], bank[:, 0 : count * COLS], TANH)
            weighted = work.tile([P, BANK_GROUPS * COLS], F32, name="weighted")
            nc.vector.tensor_tensor(
                weighted[:, 0 : count * COLS],
                squashed[:, 0 : count * COLS],
                w3_columns[:, first * COLS : (first + count) * COLS],
                MULT,
            )
            nc.vector.tensor_reduce(
                sums.rearrange("p (q a) -> p q a", q=Q)[:, :, first : first + count],
                weighted[:, 0 : count * COLS].rearrange("p (a q k) -> p q a k", a=count, q=Q),
                axis=INNERMOST,
                op=ADD,
            )

        mean_var = held.tile([N, 2], F32, name="mean_var")
        inverse_dev = held.tile([N, 1], F32, name="inverse_dev")
        constant_rows = held.tile([N, 2, P], F32, name="constant_rows")
        spread = once.tile([P, 2, N], F32, name="spread", tag="once")
        flip_of_u = BLOCKS * len(chunks) + 2

        nc.scalar.copy(
            w3_columns[:].rearrange("p (a q k) -> p a q k", a=GROUPS, q=Q),
            w3_rows[:].rearrange("p (k q a) -> p a q k", k=H2, q=Q),
        )
        for n in range(len(chunks)):
            second_layer(n)
        for n in range(len(chunks), len(stream) + LAG):
            if n < len(stream):
                first_layer(n)
            if n >= len(chunks) + LAG:
                second_layer(n - LAG)
            if n == flip_of_u:
                u_flipped = once.tile([N, T], F32, name="u_flipped", tag="once")
                nc.tensor.transpose(u_flipped[:], u[:, 0:N], identity[:])
                partial = held.tile([N, 6], F32, name="partial")
                nc.vector.bn_stats(partial[:], u_flipped[:])
                nc.vector.bn_aggr(mean_var[:], partial[:])
                nc.gpsimd.tensor_tensor(inverse_dev[:], mean_var[:, 1:2], minus_half[:], POW)
            if n == flip_of_u + 1:
                nc.vector.tensor_scalar(constant_rows[:, 0, :], ones[:], mean_var[:, 0:1], None, op0=MULT)
                nc.vector.tensor_scalar(constant_rows[:, 1, :], ones[:], inverse_dev[:, 0:1], None, op0=MULT)
        for i in range(2):
            nc.tensor.transpose(spread[:, i, :], constant_rows[:, i, :], identity[:])

        centred = held.tile([P, BLOCKS, N], F32, name="centred")
        nc.vector.tensor_tensor(
            centred[:], y[:, :, 0:N], spread[:, 0, :].unsqueeze(1).to_broadcast([P, BLOCKS, N]), SUBTRACT
        )
        standardised = held.tile([P, BLOCKS, N], F32, name="standardised")
        nc.vector.tensor_tensor(
            standardised[:], centred[:], spread[:, 1, :].unsqueeze(1).to_broadcast([P, BLOCKS, N]), MULT
        )
        nc.sync.dma_start(out.rearrange("(b p) j -> p b j", p=P), standardised[:])
